import numpy as np
import ml_dtypes


def mxq(x, axis, fmt="e4m3"):
    dtype, down = {"e4m3": (ml_dtypes.float8_e4m3fn, 7), "e5m2": (ml_dtypes.float8_e5m2, 14)}[fmt]
    v = np.moveaxis(np.asarray(x, np.float32).astype(ml_dtypes.bfloat16).astype(np.float64), axis, -1)
    blocks = v.reshape(v.shape[:-1] + (-1, 32))
    amax = np.abs(blocks).max(-1, keepdims=True)
    byte = np.maximum(np.where(amax > 0, np.frexp(amax)[1] - 1 + 127, 0) - down, 1)
    scale = np.exp2(byte - 127.0)
    codes = (blocks / scale).astype(np.float32).astype(dtype).astype(np.float64)
    return np.moveaxis((codes * scale).reshape(v.shape), -1, axis)


WIDE = False


def mx_kscale(k):
    if not WIDE:
        return np.ones(k)
    levels = np.array([10, -10, 5, -5, 0])
    a = np.random.permutation(np.resize(levels, k // 512 * 4)).reshape(k // 512, 4)
    idx = np.arange(k)
    return np.exp2(a[idx // 512, idx % 128 // 32])


BF16 = ml_dtypes.bfloat16


def bf(x):
    return np.asarray(x, np.float32).astype(BF16)


def f64(x):
    return np.asarray(x).astype(np.float64)


E2M1 = np.array([0.0, 0.5, 1.0, 1.5, 2.0, 3.0, 4.0, 6.0, -0.0, -0.5, -1.0, -1.5, -2.0, -3.0, -4.0, -6.0])


def pack_weight(w, fmt):
    k, n = w.shape
    w = f64(bf(w)).reshape(k // 32, 32, n)
    amax = np.abs(w).max(1)
    if fmt == "e4m3":
        byte = np.frexp(amax)[1] - 1 + 127 - 7
    else:
        mant, ex = np.frexp(amax / 6.0)
        byte = np.where(mant > 0.5, ex, ex - 1) + 127
    byte = np.clip(np.where(amax > 0, byte, 1), 1, 254)
    scaled = (w * np.exp2(127.0 - byte)[:, None, :]).reshape(k, n).astype(np.float32)
    by_word = np.ascontiguousarray(scaled.reshape(k // 512, 128, 4, n).transpose(0, 1, 3, 2))
    if fmt == "e4m3":
        words = by_word.astype(ml_dtypes.float8_e4m3fn).view(np.uint8)
    else:
        c = by_word.astype(ml_dtypes.float4_e2m1fn).view(np.uint8) & 0xF
        words = c[..., 0::2] | (c[..., 1::2] << 4)
    return np.ascontiguousarray(words), np.ascontiguousarray(byte.astype(np.uint8).reshape(k // 512, 16, n))


def unpack_weight(words, scales, fmt):
    g, p, n, _ = words.shape
    if fmt == "e4m3":
        vals = np.ascontiguousarray(words).view(ml_dtypes.float8_e4m3fn).astype(np.float64)
    else:
        nib = np.empty((g, p, n, 4), np.uint8)
        nib[..., 0::2] = words & 0xF
        nib[..., 1::2] = words >> 4
        vals = E2M1[nib]
    vals = vals * np.repeat(np.exp2(scales.astype(np.float64) - 127.0), 8, axis=1)[..., None]
    return vals.transpose(0, 1, 3, 2).reshape(g * 512, n)


B, N, C = 16, 16, 1024
NEG_SLOPE = 0.2
FMT = "e4m3"


def leaky(v):
    return np.where(v >= 0, v, NEG_SLOPE * v)


def setup_inputs():
    s, t = mx_kscale(C), mx_kscale(C)
    w1 = np.random.standard_normal((2, C, C)) * 0.7 / np.sqrt(C) / s[None, :, None] * t
    F = bf(np.random.standard_normal((B, N, C)) * s)
    W1_words, W1_scales = pack_weight(w1.reshape(2 * C, C), FMT)
    b1 = bf(np.random.standard_normal(C) * 0.2 * t)
    W2_words, W2_scales = pack_weight(np.random.standard_normal((C, C)) / np.sqrt(C) / t[:, None], FMT)
    b2 = bf(np.random.standard_normal(C) * 0.2)
    return {"F": F,
            "W1_words": W1_words,
            "W1_scales": W1_scales,
            "b1": b1,
            "W2_words": W2_words,
            "W2_scales": W2_scales,
            "b2": b2}


def reference(F, W1_words, W1_scales, b1, W2_words, W2_scales, b2):
    Fq = mxq(f64(F), 2, "e4m3")
    W1 = unpack_weight(W1_words, W1_scales, FMT)
    W2 = unpack_weight(W2_words, W2_scales, FMT)
    A = Fq @ W1[:C]
    Bp = Fq @ W1[C:]
    h = leaky(A[:, :, None, :] + Bp[:, None, :, :] + f64(b1))
    h = leaky((mxq(h, 3, "e4m3") @ W2) + f64(b2))
    return h.sum(-2)

@@ -1,0 +1,280 @@
+from contextlib import ExitStack
+
+import concourse.mybir as mybir
+from concourse.masks import make_identity
+
+F32 = mybir.dt.float32
+BF16 = mybir.dt.bfloat16
+I32 = mybir.dt.int32
+U32 = mybir.dt.uint32
+U8 = mybir.dt.uint8
+FP8X4 = mybir.dt.float8_e4m3fn_x4
+ACT = mybir.ActivationFunctionType
+ALU = mybir.AluOpType
+
+P = 128
+PACK = 4
+K_PASS = P * PACK
+BANK = 512
+
+SETS = 16
+NODES = 16
+C = 1024
+ROWS = SETS * NODES
+ROW_TILES = ROWS // P
+PASSES = C // K_PASS
+HALVES = C // BANK
+C_TILES = C // P
+QUAD = BANK // P
+J_STEP = BANK // ROWS
+PAIR_BLOCKS = NODES // J_STEP
+SLOPE = 0.2
+
+FLOPS = 2 * ROWS * (2 * C) * C + 2 * ROWS * NODES * C * C
+
+
+def tile_nonlocalmp_pa_kernel(tc, F, W1_words, W1_scales, b1, W2_words, W2_scales, b2, out):
+    nc = tc.nc
+    with ExitStack() as ctx:
+        ctx.enter_context(tc.manual_schedule())
+        keep = ctx.enter_context(tc.tile_pool(name="keep", bufs=1))
+        stage = ctx.enter_context(tc.tile_pool(name="stage", bufs=2))
+
+        w1_planes = keep.tile([P, C], U8, align_bytes=64)
+        w2_planes = keep.tile([P, C], U8, align_bytes=64)
+        nc.vector.memset(w1_planes[:].bitcast(I32), 0)
+        nc.vector.memset(w2_planes[:].bitcast(I32), 0)
+        w1_scale_rows = W1_scales.bitcast(I32)
+        w2_scale_rows = W2_scales.bitcast(I32)
+        for quadrant in range(4):
+            rows = slice(4 * quadrant, 4 * quadrant + 4)
+            first = 32 * quadrant
+            nc.sync.dma_start(
+                out=w1_planes[first : first + 4 * 2 * PASSES, :].bitcast(I32), in_=w1_scale_rows[:, rows, :]
+            )
+            nc.sync.dma_start(out=w2_planes[first : first + 4 * PASSES, :].bitcast(I32), in_=w2_scale_rows[:, rows, :])
+
+        f_rows = keep.tile([P, ROW_TILES, C], BF16)
+        nc.scalar.dma_start(out=f_rows[:], in_=F.flatten_outer_dims().rearrange("(r p) c -> p r c", p=P))
+        b1_all = keep.tile([P, C], BF16)
+        nc.scalar.dma_start(out=b1_all[:], in_=b1.partition_broadcast(P))
+        b2_rows = keep.tile([P, P], BF16)
+        nc.vector.memset(b2_rows[:], 0.0)
+        nc.scalar.dma_start(out=b2_rows[0:C_TILES, :], in_=b2.rearrange("(c p) -> c p", p=P))
+
+        w1_words = keep.tile([P, 2 * PASSES, C], U32, align_bytes=64)
+        w1_source = W1_words.rearrange("g p n t -> g p (n t)").bitcast(I32)
+        for half in range(HALVES):
+            cols = slice(half * BANK, (half + 1) * BANK)
+            for g in range(2 * PASSES):
+                nc.sync.dma_start(out=w1_words[:, g, cols].bitcast(I32), in_=w1_source[g, :, cols])
+        w2_words = keep.tile([P, PASSES, C], U32, align_bytes=64)
+        w2_source = W2_words.rearrange("g p n t -> g p (n t)").bitcast(I32)
+        for g in range(PASSES):
+            nc.sync.dma_start(out=w2_words[:, g, :].bitcast(I32), in_=w2_source[g])
+
+        identity = keep.tile([P, P], F32)
+        make_identity(nc, identity[:])
+
+        a_t = keep.tile([P, PASSES, SETS, NODES, PACK], F32)
+        b_t = keep.tile([P, PASSES, SETS, NODES, PACK], F32)
+        bias_steep = keep.tile([P, C_TILES], F32)
+        bias_flat = keep.tile([P, C_TILES], F32)
+
+        with tc.psum_pool(name="first_layer_banks", bufs=8) as banks:
+            f_words = f_rows[:].bitcast(F32)
+            f_codes = keep.tile([P, PASSES, ROWS], U32, align_bytes=64)
+            f_planes = keep.tile([P, PASSES, ROWS], U8, align_bytes=64)
+            f_grouped = []
+            for g in range(PASSES):
+                turned = banks.tile([P, ROW_TILES, 2, P], F32, tag="bank")
+                for r in range(ROW_TILES):
+                    for u in range(2):
+                        nc.tensor.transpose(
+                            turned[:, r, u, :], f_words[:, r, 256 * g + u : 256 * (g + 1) : 2], identity[:]
+                        )
+                grouped = stage.tile([P, ROWS * PACK], BF16, name="f_grouped", align_bytes=64)
+                nc.vector.tensor_copy(
+                    out=grouped[:].bitcast(F32).rearrange("p (r n u) -> p r n u", r=ROW_TILES, u=2),
+                    in_=turned[:].rearrange("p r u n -> p r n u"),
+                )
+                f_grouped.append(grouped)
+            for g in range(PASSES):
+                nc.vector.quantize_mx(
+                    out=f_codes[:, g, :].bitcast(FP8X4), scales=f_planes[:, g, :], in_=f_grouped[g][:]
+                )
+
+            b2_wide = keep.tile([P, P], F32)
+            nc.vector.tensor_copy(out=b2_wide[:], in_=b2_rows[:])
+            b2_turned = banks.tile([P, P], F32, tag="bank")
+            nc.tensor.transpose(b2_turned[:], b2_wide[:], identity[:])
+            nc.vector.tensor_scalar_mul(out=bias_steep[:], in0=b2_turned[:, 0:C_TILES], scalar1=1.0 - SLOPE)
+            nc.vector.tensor_scalar_mul(out=bias_flat[:], in0=b2_turned[:, 0:C_TILES], scalar1=SLOPE)
+
+            for half in range(HALVES):
+                cols = slice(half * BANK, (half + 1) * BANK)
+                sorted_rows = {}
+                for part in range(2):
+                    for r in range(ROW_TILES):
+                        m_cols = slice(r * P, (r + 1) * P)
+                        product = banks.tile([P, BANK], F32, tag="bank")
+                        for g in range(PASSES):
+                            w1_pass = PASSES * part + g
+                            nc.tensor.matmul_mx(
+                                out=product[:],
+                                lhsT=f_codes[:, g, m_cols].bitcast(FP8X4),
+                                lhsT_scale=f_planes[:, g, m_cols],
+                                rhs=w1_words[:, w1_pass, cols].bitcast(FP8X4),
+                                rhs_scale=w1_planes[4 * w1_pass : P, cols],
+                                start=(g == 0),
+                                stop=(g == PASSES - 1),
+                            )
+                        by_t = stage.tile([P, PACK, P], F32, name="by_t", bufs=8)
+                        if part == 0:
+                            nc.scalar.copy(out=by_t[:], in_=product[:].rearrange("r (p t) -> r t p", t=PACK))
+                        else:
+                            nc.vector.tensor_tensor(
+                                out=by_t[:],
+                                in0=product[:].rearrange("r (p t) -> r t p", t=PACK),
+                                in1=b1_all[:, cols].rearrange("r (p t) -> r t p", t=PACK),
+                                op=ALU.add,
+                            )
+                        sorted_rows[(part, r)] = by_t
+                for part in range(2):
+                    for r in range(ROW_TILES):
+                        turned = banks.tile([P, PACK, P], F32, tag="bank")
+                        for t in range(PACK):
+                            nc.tensor.transpose(turned[:, t, :], sorted_rows[(part, r)][:, t, :], identity[:])
+                        target = a_t if part == 0 else b_t
+                        sets = slice(r * P // NODES, (r + 1) * P // NODES)
+                        nc.scalar.copy(
+                            out=target[:, half, sets, :, :].rearrange("p b n t -> p (b n) t"),
+                            in_=turned[:].rearrange("p t n -> p n t"),
+                        )
+
+        hidden = ctx.enter_context(tc.tile_pool(name="hidden", bufs=2))
+        words = ctx.enter_context(tc.tile_pool(name="words", bufs=3))
+        pieces = ctx.enter_context(tc.tile_pool(name="pieces", bufs=2 * QUAD))
+        results = ctx.enter_context(tc.tile_pool(name="results", bufs=4))
+        product_banks = ctx.enter_context(tc.psum_pool(name="product_banks", bufs=4))
+        sum_banks = ctx.enter_context(tc.psum_pool(name="sum_banks", bufs=1))
+
+        sums = {}
+        for r in range(ROW_TILES):
+            for half in range(HALVES):
+                sums[(r, half)] = sum_banks.tile([P, BANK], F32, name="sum_%d_%d" % (r, half))
+
+        out_rows = out.flatten_outer_dims()
+        h_sum = {}
+        h_rounded = {}
+        h_words = {}
+        leaky_pieces = {}
+
+        def add_pairs(unit):
+            block, g = divmod(unit, PASSES)
+            total = hidden.tile([P, J_STEP, SETS, NODES, PACK], F32, name="h_sum")
+            for step in range(J_STEP):
+                j = block * J_STEP + step
+                nc.vector.tensor_tensor(
+                    out=total[:, step],
+                    in0=a_t[:, g],
+                    in1=b_t[:, g, :, j, :].unsqueeze(2).to_broadcast([P, SETS, NODES, PACK]),
+                    op=ALU.add,
+                )
+            h_sum[unit] = total
+
+        def leaky_and_round(unit):
+            flat = h_sum[unit][:].rearrange("p s b n t -> p (s b n t)")
+            rounded = hidden.tile([P, BANK * PACK], BF16, name="h_rounded", align_bytes=64)
+            nc.vector.scalar_tensor_tensor(out=rounded[:], in0=flat, scalar=SLOPE, in1=flat, op0=ALU.mult, op1=ALU.max)
+            h_rounded[unit] = rounded
+
+        def quantise(unit):
+            block, g = divmod(unit, PASSES)
+            if g == 0:
+                codes = words.tile([P, PASSES, BANK], U32, name="h_codes", align_bytes=64)
+                planes = words.tile([P, PASSES, BANK], U8, name="h_planes", align_bytes=64)
+                h_words[block] = (codes, planes)
+            codes, planes = h_words[block]
+            nc.vector.quantize_mx(out=codes[:, g, :].bitcast(FP8X4), scales=planes[:, g, :], in_=h_rounded[unit][:])
+
+        def multiply(block, half):
+            codes, planes = h_words[block]
+            done = []
+            for c_tile in range(half * QUAD, (half + 1) * QUAD):
+                m_cols = slice(c_tile * P, (c_tile + 1) * P)
+                product = product_banks.tile([P, BANK], F32, name="product")
+                for g in range(PASSES):
+                    nc.tensor.matmul_mx(
+                        out=product[:],
+                        lhsT=w2_words[:, g, m_cols].bitcast(FP8X4),
+                        lhsT_scale=w2_planes[4 * g : P, m_cols],
+                        rhs=codes[:, g, :].bitcast(FP8X4),
+                        rhs_scale=planes[:, g, :],
+                        start=(g == 0),
+                        stop=(g == PASSES - 1),
+                    )
+                steep = pieces.tile([P, BANK], F32, name="steep")
+                flat = pieces.tile([P, BANK], F32, name="flat")
+                nc.scalar.activation(
+                    out=steep[:], in_=product[:], func=ACT.Relu, bias=bias_steep[:, c_tile : c_tile + 1], scale=1.0 - SLOPE
+                )
+                nc.scalar.activation(
+                    out=flat[:], in_=product[:], func=ACT.Identity, bias=bias_flat[:, c_tile : c_tile + 1], scale=SLOPE
+                )
+                done.append((c_tile, steep, flat))
+            leaky_pieces[(block, half)] = done
+
+        def add_up(block, half):
+            for c_tile, steep, flat in leaky_pieces[(block, half)]:
+                n_cols = slice((c_tile % QUAD) * P, (c_tile % QUAD + 1) * P)
+                for step in range(J_STEP):
+                    for r in range(ROW_TILES):
+                        pair_cols = slice((step * ROW_TILES + r) * P, (step * ROW_TILES + r + 1) * P)
+                        opens = block == 0 and c_tile % QUAD == 0 and step == 0
+                        closes = block == PAIR_BLOCKS - 1 and c_tile % QUAD == QUAD - 1 and step == J_STEP - 1
+                        nc.tensor.matmul(
+                            out=sums[(r, half)][:, n_cols],
+                            lhsT=steep[:, pair_cols],
+                            rhs=identity[:],
+                            is_transpose=True,
+                            start=opens,
+                            stop=False,
+                        )
+                        nc.tensor.matmul(
+                            out=sums[(r, half)][:, n_cols],
+                            lhsT=flat[:, pair_cols],
+                            rhs=identity[:],
+                            is_transpose=True,
+                            start=False,
+                            stop=closes,
+                        )
+
+        def store(half):
+            for r in range(ROW_TILES):
+                result = results.tile([P, BANK], F32, name="result")
+                if r == 0:
+                    nc.vector.tensor_copy(out=result[:], in_=sums[(r, half)][:])
+                else:
+                    nc.scalar.copy(out=result[:], in_=sums[(r, half)][:])
+                nc.sync.dma_start(out=out_rows[r * P : (r + 1) * P, half * BANK : (half + 1) * BANK], in_=result[:])
+
+        rounds = [(block, half) for block in range(PAIR_BLOCKS) for half in range(HALVES)]
+        units = PAIR_BLOCKS * PASSES
+        for unit in range(units + 1):
+            if unit < units:
+                add_pairs(unit)
+            if unit > 0:
+                quantise(unit - 1)
+            if unit < units:
+                leaky_and_round(unit)
+            if unit > 0 and unit % PASSES == 0:
+                block = unit // PASSES - 1
+                for half in range(HALVES):
+                    multiply(block, half)
+                    before = rounds.index((block, half)) - 1
+                    if before >= 0:
+                        add_up(*rounds[before])
+        store(0)
+        add_up(*rounds[-1])
+        store(1)

@@ -26,8 +26,8 @@ PASSES = C // K_PASS
 HALVES = C // BANK
 C_TILES = C // P
 QUAD = BANK // P
-J_STEP = BANK // ROWS
-PAIR_BLOCKS = NODES // J_STEP
+TILES_A_BANK = BANK // ROWS
+PRODUCT_BANKS = C_TILES // TILES_A_BANK
 SLOPE = 0.2
 
 FLOPS = 2 * ROWS * (2 * C) * C + 2 * ROWS * NODES * C * C
@@ -44,34 +44,35 @@ def tile_nonlocalmp_pa_kernel(tc, F, W1_words, W1_scales, b1, W2_words, W2_scale
         w2_planes = keep.tile([P, C], U8, align_bytes=64)
         nc.vector.memset(w1_planes[:].bitcast(I32), 0)
         nc.vector.memset(w2_planes[:].bitcast(I32), 0)
-        w1_scale_rows = W1_scales.bitcast(I32)
-        w2_scale_rows = W2_scales.bitcast(I32)
-        for quadrant in range(4):
-            rows = slice(4 * quadrant, 4 * quadrant + 4)
-            first = 32 * quadrant
-            nc.sync.dma_start(
-                out=w1_planes[first : first + 4 * 2 * PASSES, :].bitcast(I32), in_=w1_scale_rows[:, rows, :]
-            )
-            nc.sync.dma_start(out=w2_planes[first : first + 4 * PASSES, :].bitcast(I32), in_=w2_scale_rows[:, rows, :])
 
         f_rows = keep.tile([P, ROW_TILES, C], BF16)
         nc.scalar.dma_start(out=f_rows[:], in_=F.flatten_outer_dims().rearrange("(r p) c -> p r c", p=P))
-        b1_all = keep.tile([P, C], BF16)
-        nc.scalar.dma_start(out=b1_all[:], in_=b1.partition_broadcast(P))
+
+        def load_planes(planes, scales, passes):
+            scale_rows = scales.bitcast(I32)
+            for quadrant in range(4):
+                first = 32 * quadrant
+                nc.sync.dma_start(
+                    out=planes[first : first + 4 * passes, :].bitcast(I32),
+                    in_=scale_rows[:, 4 * quadrant : 4 * quadrant + 4, :],
+                )
+
+        load_planes(w1_planes, W1_scales, 2 * PASSES)
+        w1_words = keep.tile([P, 2 * PASSES, C], U32, align_bytes=64)
+        w1_source = W1_words.rearrange("g p n t -> p g (n t)").bitcast(I32)
+        for half in range(HALVES):
+            cols = slice(half * BANK, (half + 1) * BANK)
+            nc.sync.dma_start(out=w1_words[:, :, cols].bitcast(I32), in_=w1_source[:, :, cols])
+
+        b1_t = keep.tile([P, PASSES, PACK], BF16)
+        nc.scalar.dma_start(out=b1_t[:], in_=b1.rearrange("(g p t) -> p g t", p=P, t=PACK))
         b2_rows = keep.tile([P, P], BF16)
         nc.vector.memset(b2_rows[:], 0.0)
         nc.scalar.dma_start(out=b2_rows[0:C_TILES, :], in_=b2.rearrange("(c p) -> c p", p=P))
 
-        w1_words = keep.tile([P, 2 * PASSES, C], U32, align_bytes=64)
-        w1_source = W1_words.rearrange("g p n t -> g p (n t)").bitcast(I32)
-        for half in range(HALVES):
-            cols = slice(half * BANK, (half + 1) * BANK)
-            for g in range(2 * PASSES):
-                nc.sync.dma_start(out=w1_words[:, g, cols].bitcast(I32), in_=w1_source[g, :, cols])
+        load_planes(w2_planes, W2_scales, PASSES)
         w2_words = keep.tile([P, PASSES, C], U32, align_bytes=64)
-        w2_source = W2_words.rearrange("g p n t -> g p (n t)").bitcast(I32)
-        for g in range(PASSES):
-            nc.sync.dma_start(out=w2_words[:, g, :].bitcast(I32), in_=w2_source[g])
+        nc.sync.dma_start(out=w2_words[:].bitcast(I32), in_=W2_words.rearrange("g p n t -> p g (n t)").bitcast(I32))
 
         identity = keep.tile([P, P], F32)
         make_identity(nc, identity[:])
@@ -103,60 +104,61 @@ def tile_nonlocalmp_pa_kernel(tc, F, W1_words, W1_scales, b1, W2_words, W2_scale
                 nc.vector.quantize_mx(
                     out=f_codes[:, g, :].bitcast(FP8X4), scales=f_planes[:, g, :], in_=f_grouped[g][:]
                 )
-
             b2_wide = keep.tile([P, P], F32)
-            nc.vector.tensor_copy(out=b2_wide[:], in_=b2_rows[:])
+            nc.scalar.copy(out=b2_wide[:], in_=b2_rows[:])
+
+            pieces_of_layer = [(half, part, r) for half in range(HALVES) for part in range(2) for r in range(ROW_TILES)]
+            sorted_rows = {}
+            for half, part, r in pieces_of_layer:
+                cols = slice(half * BANK, (half + 1) * BANK)
+                m_cols = slice(r * P, (r + 1) * P)
+                product = banks.tile([P, BANK], F32, tag="bank")
+                for g in range(PASSES):
+                    w1_pass = PASSES * part + g
+                    nc.tensor.matmul_mx(
+                        out=product[:],
+                        lhsT=f_codes[:, g, m_cols].bitcast(FP8X4),
+                        lhsT_scale=f_planes[:, g, m_cols],
+                        rhs=w1_words[:, w1_pass, cols].bitcast(FP8X4),
+                        rhs_scale=w1_planes[4 * w1_pass : P, cols],
+                        start=(g == 0),
+                        stop=(g == PASSES - 1),
+                    )
+                by_t = stage.tile([P, PACK, P], F32, name="by_t", bufs=len(pieces_of_layer))
+                if part == 0:
+                    nc.scalar.copy(out=by_t[:], in_=product[:].rearrange("r (p t) -> r t p", t=PACK))
+                else:
+                    nc.vector.tensor_copy(out=by_t[:], in_=product[:].rearrange("r (p t) -> r t p", t=PACK))
+                sorted_rows[(half, part, r)] = by_t
+
             b2_turned = banks.tile([P, P], F32, tag="bank")
             nc.tensor.transpose(b2_turned[:], b2_wide[:], identity[:])
-            nc.vector.tensor_scalar_mul(out=bias_steep[:], in0=b2_turned[:, 0:C_TILES], scalar1=1.0 - SLOPE)
-            nc.vector.tensor_scalar_mul(out=bias_flat[:], in0=b2_turned[:, 0:C_TILES], scalar1=SLOPE)
+            nc.scalar.mul(out=bias_steep[:], in_=b2_turned[:, 0:C_TILES], mul=1.0 - SLOPE)
+            nc.scalar.mul(out=bias_flat[:], in_=b2_turned[:, 0:C_TILES], mul=SLOPE)
 
-            for half in range(HALVES):
-                cols = slice(half * BANK, (half + 1) * BANK)
-                sorted_rows = {}
-                for part in range(2):
-                    for r in range(ROW_TILES):
-                        m_cols = slice(r * P, (r + 1) * P)
-                        product = banks.tile([P, BANK], F32, tag="bank")
-                        for g in range(PASSES):
-                            w1_pass = PASSES * part + g
-                            nc.tensor.matmul_mx(
-                                out=product[:],
-                                lhsT=f_codes[:, g, m_cols].bitcast(FP8X4),
-                                lhsT_scale=f_planes[:, g, m_cols],
-                                rhs=w1_words[:, w1_pass, cols].bitcast(FP8X4),
-                                rhs_scale=w1_planes[4 * w1_pass : P, cols],
-                                start=(g == 0),
-                                stop=(g == PASSES - 1),
-                            )
-                        by_t = stage.tile([P, PACK, P], F32, name="by_t", bufs=8)
-                        if part == 0:
-                            nc.scalar.copy(out=by_t[:], in_=product[:].rearrange("r (p t) -> r t p", t=PACK))
-                        else:
-                            nc.vector.tensor_tensor(
-                                out=by_t[:],
-                                in0=product[:].rearrange("r (p t) -> r t p", t=PACK),
-                                in1=b1_all[:, cols].rearrange("r (p t) -> r t p", t=PACK),
-                                op=ALU.add,
-                            )
-                        sorted_rows[(part, r)] = by_t
-                for part in range(2):
-                    for r in range(ROW_TILES):
-                        turned = banks.tile([P, PACK, P], F32, tag="bank")
-                        for t in range(PACK):
-                            nc.tensor.transpose(turned[:, t, :], sorted_rows[(part, r)][:, t, :], identity[:])
-                        target = a_t if part == 0 else b_t
-                        sets = slice(r * P // NODES, (r + 1) * P // NODES)
-                        nc.scalar.copy(
-                            out=target[:, half, sets, :, :].rearrange("p b n t -> p (b n) t"),
-                            in_=turned[:].rearrange("p t n -> p n t"),
-                        )
+            for half, part, r in pieces_of_layer:
+                turned = banks.tile([P, PACK, P], F32, tag="bank")
+                for t in range(PACK):
+                    nc.tensor.transpose(turned[:, t, :], sorted_rows[(half, part, r)][:, t, :], identity[:])
+                sets = slice(r * P // NODES, (r + 1) * P // NODES)
+                if part == 0:
+                    nc.scalar.copy(
+                        out=a_t[:, half, sets, :, :].rearrange("p b n t -> p (b n) t"),
+                        in_=turned[:].rearrange("p t n -> p n t"),
+                    )
+                else:
+                    nc.vector.tensor_tensor(
+                        out=b_t[:, half, sets, :, :].rearrange("p b n t -> p (b n) t"),
+                        in0=turned[:].rearrange("p t n -> p n t"),
+                        in1=b1_t[:, half, :].unsqueeze(1).to_broadcast([P, P, PACK]),
+                        op=ALU.add,
+                    )
 
         hidden = ctx.enter_context(tc.tile_pool(name="hidden", bufs=2))
-        words = ctx.enter_context(tc.tile_pool(name="words", bufs=3))
-        pieces = ctx.enter_context(tc.tile_pool(name="pieces", bufs=2 * QUAD))
-        results = ctx.enter_context(tc.tile_pool(name="results", bufs=4))
-        product_banks = ctx.enter_context(tc.psum_pool(name="product_banks", bufs=4))
+        words = ctx.enter_context(tc.tile_pool(name="words", bufs=4))
+        pieces = ctx.enter_context(tc.tile_pool(name="pieces", bufs=2 * PRODUCT_BANKS))
+        results = ctx.enter_context(tc.tile_pool(name="results", bufs=ROW_TILES * HALVES))
+        product_banks = ctx.enter_context(tc.psum_pool(name="product_banks", bufs=PRODUCT_BANKS))
         sum_banks = ctx.enter_context(tc.psum_pool(name="sum_banks", bufs=1))
 
         sums = {}
@@ -171,96 +173,97 @@ def tile_nonlocalmp_pa_kernel(tc, F, W1_words, W1_scales, b1, W2_words, W2_scale
         leaky_pieces = {}
 
         def add_pairs(unit):
-            block, g = divmod(unit, PASSES)
-            total = hidden.tile([P, J_STEP, SETS, NODES, PACK], F32, name="h_sum")
-            for step in range(J_STEP):
-                j = block * J_STEP + step
-                nc.vector.tensor_tensor(
-                    out=total[:, step],
-                    in0=a_t[:, g],
-                    in1=b_t[:, g, :, j, :].unsqueeze(2).to_broadcast([P, SETS, NODES, PACK]),
-                    op=ALU.add,
-                )
+            j, g = divmod(unit, PASSES)
+            total = hidden.tile([P, SETS, NODES, PACK], F32, name="h_sum")
+            nc.vector.tensor_tensor(
+                out=total[:],
+                in0=a_t[:, g],
+                in1=b_t[:, g, :, j, :].unsqueeze(2).to_broadcast([P, SETS, NODES, PACK]),
+                op=ALU.add,
+            )
             h_sum[unit] = total
 
         def leaky_and_round(unit):
-            flat = h_sum[unit][:].rearrange("p s b n t -> p (s b n t)")
-            rounded = hidden.tile([P, BANK * PACK], BF16, name="h_rounded", align_bytes=64)
-            nc.vector.scalar_tensor_tensor(out=rounded[:], in0=flat, scalar=SLOPE, in1=flat, op0=ALU.mult, op1=ALU.max)
+            total = h_sum[unit][:].rearrange("p b n t -> p (b n t)")
+            rounded = hidden.tile([P, ROWS * PACK], BF16, name="h_rounded", align_bytes=64)
+            nc.vector.scalar_tensor_tensor(
+                out=rounded[:], in0=total, scalar=SLOPE, in1=total, op0=ALU.mult, op1=ALU.max
+            )
             h_rounded[unit] = rounded
 
         def quantise(unit):
-            block, g = divmod(unit, PASSES)
+            j, g = divmod(unit, PASSES)
             if g == 0:
-                codes = words.tile([P, PASSES, BANK], U32, name="h_codes", align_bytes=64)
-                planes = words.tile([P, PASSES, BANK], U8, name="h_planes", align_bytes=64)
-                h_words[block] = (codes, planes)
-            codes, planes = h_words[block]
+                codes = words.tile([P, PASSES, ROWS], U32, name="h_codes", align_bytes=64)
+                planes = words.tile([P, PASSES, ROWS], U8, name="h_planes", align_bytes=64)
+                h_words[j] = (codes, planes)
+            codes, planes = h_words[j]
             nc.vector.quantize_mx(out=codes[:, g, :].bitcast(FP8X4), scales=planes[:, g, :], in_=h_rounded[unit][:])
 
-        def multiply(block, half):
-            codes, planes = h_words[block]
-            done = []
-            for c_tile in range(half * QUAD, (half + 1) * QUAD):
-                m_cols = slice(c_tile * P, (c_tile + 1) * P)
-                product = product_banks.tile([P, BANK], F32, name="product")
-                for g in range(PASSES):
-                    nc.tensor.matmul_mx(
-                        out=product[:],
-                        lhsT=w2_words[:, g, m_cols].bitcast(FP8X4),
-                        lhsT_scale=w2_planes[4 * g : P, m_cols],
-                        rhs=codes[:, g, :].bitcast(FP8X4),
-                        rhs_scale=planes[:, g, :],
-                        start=(g == 0),
-                        stop=(g == PASSES - 1),
+        def multiply(j):
+            codes, planes = h_words[j]
+            leaky_pieces[j] = []
+            for bank in range(PRODUCT_BANKS):
+                product = product_banks.tile([P, TILES_A_BANK, ROWS], F32, name="product")
+                steep = pieces.tile([P, TILES_A_BANK, ROWS], F32, name="steep")
+                flat = pieces.tile([P, TILES_A_BANK, ROWS], F32, name="flat")
+                for k in range(TILES_A_BANK):
+                    c_tile = bank * TILES_A_BANK + k
+                    m_cols = slice(c_tile * P, (c_tile + 1) * P)
+                    for g in range(PASSES):
+                        nc.tensor.matmul_mx(
+                            out=product[:, k, :],
+                            lhsT=w2_words[:, g, m_cols].bitcast(FP8X4),
+                            lhsT_scale=w2_planes[4 * g : P, m_cols],
+                            rhs=codes[:, g, :].bitcast(FP8X4),
+                            rhs_scale=planes[:, g, :],
+                            start=(g == 0),
+                            stop=(g == PASSES - 1),
+                        )
+                for k in range(TILES_A_BANK):
+                    c_tile = bank * TILES_A_BANK + k
+                    nc.scalar.activation(
+                        out=steep[:, k, :],
+                        in_=product[:, k, :],
+                        func=ACT.Relu,
+                        bias=bias_steep[:, c_tile : c_tile + 1],
+                        scale=1.0 - SLOPE,
                     )
-                steep = pieces.tile([P, BANK], F32, name="steep")
-                flat = pieces.tile([P, BANK], F32, name="flat")
-                nc.scalar.activation(
-                    out=steep[:], in_=product[:], func=ACT.Relu, bias=bias_steep[:, c_tile : c_tile + 1], scale=1.0 - SLOPE
-                )
-                nc.scalar.activation(
-                    out=flat[:], in_=product[:], func=ACT.Identity, bias=bias_flat[:, c_tile : c_tile + 1], scale=SLOPE
-                )
-                done.append((c_tile, steep, flat))
-            leaky_pieces[(block, half)] = done
+                    nc.scalar.activation(
+                        out=flat[:, k, :],
+                        in_=product[:, k, :],
+                        func=ACT.Identity,
+                        bias=bias_flat[:, c_tile : c_tile + 1],
+                        scale=SLOPE,
+                    )
+                leaky_pieces[j].append((steep, flat))
 
-        def add_up(block, half):
-            for c_tile, steep, flat in leaky_pieces[(block, half)]:
-                n_cols = slice((c_tile % QUAD) * P, (c_tile % QUAD + 1) * P)
-                for step in range(J_STEP):
-                    for r in range(ROW_TILES):
-                        pair_cols = slice((step * ROW_TILES + r) * P, (step * ROW_TILES + r + 1) * P)
-                        opens = block == 0 and c_tile % QUAD == 0 and step == 0
-                        closes = block == PAIR_BLOCKS - 1 and c_tile % QUAD == QUAD - 1 and step == J_STEP - 1
-                        nc.tensor.matmul(
-                            out=sums[(r, half)][:, n_cols],
-                            lhsT=steep[:, pair_cols],
-                            rhs=identity[:],
-                            is_transpose=True,
-                            start=opens,
-                            stop=False,
-                        )
-                        nc.tensor.matmul(
-                            out=sums[(r, half)][:, n_cols],
-                            lhsT=flat[:, pair_cols],
-                            rhs=identity[:],
-                            is_transpose=True,
-                            start=False,
-                            stop=closes,
-                        )
+        def add_up(j):
+            for c_tile in range(C_TILES):
+                bank, k = divmod(c_tile, TILES_A_BANK)
+                half, quarter = divmod(c_tile, QUAD)
+                steep, flat = leaky_pieces[j][bank]
+                for r in range(ROW_TILES):
+                    target = sums[(r, half)][:, quarter * P : (quarter + 1) * P]
+                    pair_cols = slice(r * P, (r + 1) * P)
+                    nc.tensor.matmul(
+                        out=target,
+                        lhsT=steep[:, k, pair_cols],
+                        rhs=identity[:],
+                        is_transpose=True,
+                        start=(j == 0 and quarter == 0),
+                        stop=False,
+                    )
+                    nc.tensor.matmul(
+                        out=target,
+                        lhsT=flat[:, k, pair_cols],
+                        rhs=identity[:],
+                        is_transpose=True,
+                        start=False,
+                        stop=(j == NODES - 1 and quarter == QUAD - 1),
+                    )
 
-        def store(half):
-            for r in range(ROW_TILES):
-                result = results.tile([P, BANK], F32, name="result")
-                if r == 0:
-                    nc.vector.tensor_copy(out=result[:], in_=sums[(r, half)][:])
-                else:
-                    nc.scalar.copy(out=result[:], in_=sums[(r, half)][:])
-                nc.sync.dma_start(out=out_rows[r * P : (r + 1) * P, half * BANK : (half + 1) * BANK], in_=result[:])
-
-        rounds = [(block, half) for block in range(PAIR_BLOCKS) for half in range(HALVES)]
-        units = PAIR_BLOCKS * PASSES
+        units = NODES * PASSES
         for unit in range(units + 1):
             if unit < units:
                 add_pairs(unit)
@@ -269,12 +272,17 @@ def tile_nonlocalmp_pa_kernel(tc, F, W1_words, W1_scales, b1, W2_words, W2_scale
             if unit < units:
                 leaky_and_round(unit)
             if unit > 0 and unit % PASSES == 0:
-                block = unit // PASSES - 1
-                for half in range(HALVES):
-                    multiply(block, half)
-                    before = rounds.index((block, half)) - 1
-                    if before >= 0:
-                        add_up(*rounds[before])
-        store(0)
-        add_up(*rounds[-1])
-        store(1)
+                j = unit // PASSES - 1
+                multiply(j)
+                if j > 0:
+                    add_up(j - 1)
+        add_up(NODES - 1)
+
+        for half in range(HALVES):
+            for r in range(ROW_TILES):
+                result = results.tile([P, BANK], F32, name="result")
+                if r == 0:
+                    nc.vector.tensor_copy(out=result[:], in_=sums[(r, half)][:])
+                else:
+                    nc.scalar.copy(out=result[:], in_=sums[(r, half)][:])
+                nc.sync.dma_start(out=out_rows[r * P : (r + 1) * P, half * BANK : (half + 1) * BANK], in_=result[:])

@@ -81,96 +81,14 @@ def tile_nonlocalmp_pa_kernel(tc, F, W1_words, W1_scales, b1, W2_words, W2_scale
         b_t = keep.tile([P, PASSES, SETS, NODES, PACK], F32)
         bias_steep = keep.tile([P, C_TILES], F32)
         bias_flat = keep.tile([P, C_TILES], F32)
+        bias_whole = keep.tile([P, C_TILES], F32)
 
-        with tc.psum_pool(name="first_layer_banks", bufs=8) as banks:
-            f_words = f_rows[:].bitcast(F32)
-            f_codes = keep.tile([P, PASSES, ROWS], U32, align_bytes=64)
-            f_planes = keep.tile([P, PASSES, ROWS], U8, align_bytes=64)
-            f_grouped = []
-            for g in range(PASSES):
-                turned = banks.tile([P, ROW_TILES, 2, P], F32, tag="bank")
-                for r in range(ROW_TILES):
-                    for u in range(2):
-                        nc.tensor.transpose(
-                            turned[:, r, u, :], f_words[:, r, 256 * g + u : 256 * (g + 1) : 2], identity[:]
-                        )
-                grouped = stage.tile([P, ROWS * PACK], BF16, name="f_grouped", align_bytes=64)
-                nc.vector.tensor_copy(
-                    out=grouped[:].bitcast(F32).rearrange("p (r n u) -> p r n u", r=ROW_TILES, u=2),
-                    in_=turned[:].rearrange("p r u n -> p r n u"),
-                )
-                f_grouped.append(grouped)
-            for g in range(PASSES):
-                nc.vector.quantize_mx(
-                    out=f_codes[:, g, :].bitcast(FP8X4), scales=f_planes[:, g, :], in_=f_grouped[g][:]
-                )
-            b2_wide = keep.tile([P, P], F32)
-            nc.scalar.copy(out=b2_wide[:], in_=b2_rows[:])
-
-            pieces_of_layer = [(half, part, r) for half in range(HALVES) for part in range(2) for r in range(ROW_TILES)]
-            sorted_rows = {}
-            for half, part, r in pieces_of_layer:
-                cols = slice(half * BANK, (half + 1) * BANK)
-                m_cols = slice(r * P, (r + 1) * P)
-                product = banks.tile([P, BANK], F32, tag="bank")
-                for g in range(PASSES):
-                    w1_pass = PASSES * part + g
-                    nc.tensor.matmul_mx(
-                        out=product[:],
-                        lhsT=f_codes[:, g, m_cols].bitcast(FP8X4),
-                        lhsT_scale=f_planes[:, g, m_cols],
-                        rhs=w1_words[:, w1_pass, cols].bitcast(FP8X4),
-                        rhs_scale=w1_planes[4 * w1_pass : P, cols],
-                        start=(g == 0),
-                        stop=(g == PASSES - 1),
-                    )
-                by_t = stage.tile([P, PACK, P], F32, name="by_t", bufs=len(pieces_of_layer))
-                if part == 0:
-                    nc.scalar.copy(out=by_t[:], in_=product[:].rearrange("r (p t) -> r t p", t=PACK))
-                else:
-                    nc.vector.tensor_copy(out=by_t[:], in_=product[:].rearrange("r (p t) -> r t p", t=PACK))
-                sorted_rows[(half, part, r)] = by_t
-
-            b2_turned = banks.tile([P, P], F32, tag="bank")
-            nc.tensor.transpose(b2_turned[:], b2_wide[:], identity[:])
-            nc.scalar.mul(out=bias_steep[:], in_=b2_turned[:, 0:C_TILES], mul=1.0 - SLOPE)
-            nc.scalar.mul(out=bias_flat[:], in_=b2_turned[:, 0:C_TILES], mul=SLOPE)
-
-            for half, part, r in pieces_of_layer:
-                turned = banks.tile([P, PACK, P], F32, tag="bank")
-                for t in range(PACK):
-                    nc.tensor.transpose(turned[:, t, :], sorted_rows[(half, part, r)][:, t, :], identity[:])
-                sets = slice(r * P // NODES, (r + 1) * P // NODES)
-                if part == 0:
-                    nc.scalar.copy(
-                        out=a_t[:, half, sets, :, :].rearrange("p b n t -> p (b n) t"),
-                        in_=turned[:].rearrange("p t n -> p n t"),
-                    )
-                else:
-                    nc.vector.tensor_tensor(
-                        out=b_t[:, half, sets, :, :].rearrange("p b n t -> p (b n) t"),
-                        in0=turned[:].rearrange("p t n -> p n t"),
-                        in1=b1_t[:, half, :].unsqueeze(1).to_broadcast([P, P, PACK]),
-                        op=ALU.add,
-                    )
 
         hidden = ctx.enter_context(tc.tile_pool(name="hidden", bufs=2))
         words = ctx.enter_context(tc.tile_pool(name="words", bufs=4))
-        pieces = ctx.enter_context(tc.tile_pool(name="pieces", bufs=2 * PRODUCT_BANKS))
-        results = ctx.enter_context(tc.tile_pool(name="results", bufs=ROW_TILES * HALVES))
-        product_banks = ctx.enter_context(tc.psum_pool(name="product_banks", bufs=PRODUCT_BANKS))
-        sum_banks = ctx.enter_context(tc.psum_pool(name="sum_banks", bufs=1))
-
-        sums = {}
-        for r in range(ROW_TILES):
-            for half in range(HALVES):
-                sums[(r, half)] = sum_banks.tile([P, BANK], F32, name="sum_%d_%d" % (r, half))
-
-        out_rows = out.flatten_outer_dims()
         h_sum = {}
         h_rounded = {}
         h_words = {}
-        leaky_pieces = {}
 
         def add_pairs(unit):
             j, g = divmod(unit, PASSES)
@@ -200,7 +118,98 @@ def tile_nonlocalmp_pa_kernel(tc, F, W1_words, W1_scales, b1, W2_words, W2_scale
             codes, planes = h_words[j]
             nc.vector.quantize_mx(out=codes[:, g, :].bitcast(FP8X4), scales=planes[:, g, :], in_=h_rounded[unit][:])
 
-        def multiply(j):
+        with tc.psum_pool(name="first_layer_banks", bufs=8) as banks:
+            f_words = f_rows[:].bitcast(F32)
+            f_codes = keep.tile([P, PASSES, ROWS], U32, align_bytes=64)
+            f_planes = keep.tile([P, PASSES, ROWS], U8, align_bytes=64)
+            f_grouped = []
+            for g in range(PASSES):
+                turned = banks.tile([P, ROW_TILES, 2, P], F32, tag="bank")
+                for r in range(ROW_TILES):
+                    for u in range(2):
+                        nc.tensor.transpose(
+                            turned[:, r, u, :], f_words[:, r, 256 * g + u : 256 * (g + 1) : 2], identity[:]
+                        )
+                grouped = stage.tile([P, ROWS * PACK], BF16, name="f_grouped", align_bytes=64)
+                nc.vector.tensor_copy(
+                    out=grouped[:].bitcast(F32).rearrange("p (r n u) -> p r n u", r=ROW_TILES, u=2),
+                    in_=turned[:].rearrange("p r u n -> p r n u"),
+                )
+                f_grouped.append(grouped)
+            for g in range(PASSES):
+                nc.vector.quantize_mx(
+                    out=f_codes[:, g, :].bitcast(FP8X4), scales=f_planes[:, g, :], in_=f_grouped[g][:]
+                )
+            b2_wide = keep.tile([P, P], F32)
+            nc.scalar.copy(out=b2_wide[:], in_=b2_rows[:])
+
+
+            for half in range(HALVES):
+                cols = slice(half * BANK, (half + 1) * BANK)
+                pieces_of_half = [(part, r) for part in range(2) for r in range(ROW_TILES)]
+                sorted_rows = {}
+                for part, r in pieces_of_half:
+                    m_cols = slice(r * P, (r + 1) * P)
+                    product = banks.tile([P, BANK], F32, tag="bank")
+                    for g in range(PASSES):
+                        w1_pass = PASSES * part + g
+                        nc.tensor.matmul_mx(
+                            out=product[:],
+                            lhsT=f_codes[:, g, m_cols].bitcast(FP8X4),
+                            lhsT_scale=f_planes[:, g, m_cols],
+                            rhs=w1_words[:, w1_pass, cols].bitcast(FP8X4),
+                            rhs_scale=w1_planes[4 * w1_pass : P, cols],
+                            start=(g == 0),
+                            stop=(g == PASSES - 1),
+                        )
+                    by_t = stage.tile([P, PACK, P], F32, name="by_t", bufs=2 * len(pieces_of_half))
+                    if part == 0 or half == 1:
+                        nc.scalar.copy(out=by_t[:], in_=product[:].rearrange("r (p t) -> r t p", t=PACK))
+                    else:
+                        nc.vector.tensor_copy(out=by_t[:], in_=product[:].rearrange("r (p t) -> r t p", t=PACK))
+                    sorted_rows[(part, r)] = by_t
+
+                for part, r in pieces_of_half:
+                    turned = banks.tile([P, PACK, P], F32, tag="bank")
+                    for t in range(PACK):
+                        nc.tensor.transpose(turned[:, t, :], sorted_rows[(part, r)][:, t, :], identity[:])
+                    sets = slice(r * P // NODES, (r + 1) * P // NODES)
+                    if part == 0:
+                        nc.scalar.copy(
+                            out=a_t[:, half, sets, :, :].rearrange("p b n t -> p (b n) t"),
+                            in_=turned[:].rearrange("p t n -> p n t"),
+                        )
+                    else:
+                        nc.vector.tensor_tensor(
+                            out=b_t[:, half, sets, :, :].rearrange("p b n t -> p (b n) t"),
+                            in0=turned[:].rearrange("p t n -> p n t"),
+                            in1=b1_t[:, half, :].unsqueeze(1).to_broadcast([P, P, PACK]),
+                            op=ALU.add,
+                        )
+                if half == 0:
+                    add_pairs(0)
+                    leaky_and_round(0)
+
+            b2_turned = banks.tile([P, P], F32, tag="bank")
+            nc.tensor.transpose(b2_turned[:], b2_wide[:], identity[:])
+            nc.scalar.mul(out=bias_steep[:], in_=b2_turned[:, 0:C_TILES], mul=1.0 - SLOPE)
+            nc.scalar.mul(out=bias_flat[:], in_=b2_turned[:, 0:C_TILES], mul=SLOPE)
+            nc.scalar.copy(out=bias_whole[:], in_=b2_turned[:, 0:C_TILES])
+
+        pieces = ctx.enter_context(tc.tile_pool(name="pieces", bufs=2 * PRODUCT_BANKS))
+        results = ctx.enter_context(tc.tile_pool(name="results", bufs=ROW_TILES * HALVES))
+        product_banks = ctx.enter_context(tc.psum_pool(name="product_banks", bufs=PRODUCT_BANKS))
+        sum_banks = ctx.enter_context(tc.psum_pool(name="sum_banks", bufs=1))
+
+        sums = {}
+        for r in range(ROW_TILES):
+            for half in range(HALVES):
+                sums[(r, half)] = sum_banks.tile([P, BANK], F32, name="sum_%d_%d" % (r, half))
+
+        out_rows = out.flatten_outer_dims()
+        leaky_pieces = {}
+
+        def multiply(j, one_piece):
             codes, planes = h_words[j]
             leaky_pieces[j] = []
             for bank in range(PRODUCT_BANKS):
@@ -223,57 +232,69 @@ def tile_nonlocalmp_pa_kernel(tc, F, W1_words, W1_scales, b1, W2_words, W2_scale
                 for k in range(TILES_A_BANK):
                     c_tile = bank * TILES_A_BANK + k
                     nc.scalar.activation(
-                        out=steep[:, k, :],
-                        in_=product[:, k, :],
-                        func=ACT.Relu,
-                        bias=bias_steep[:, c_tile : c_tile + 1],
-                        scale=1.0 - SLOPE,
-                    )
-                    nc.scalar.activation(
                         out=flat[:, k, :],
                         in_=product[:, k, :],
                         func=ACT.Identity,
                         bias=bias_flat[:, c_tile : c_tile + 1],
                         scale=SLOPE,
                     )
-                leaky_pieces[j].append((steep, flat))
+                for k in range(TILES_A_BANK):
+                    c_tile = bank * TILES_A_BANK + k
+                    if one_piece:
+                        nc.vector.scalar_tensor_tensor(
+                            out=steep[:, k, :],
+                            in0=product[:, k, :],
+                            scalar=bias_whole[:, c_tile : c_tile + 1],
+                            in1=flat[:, k, :],
+                            op0=ALU.add,
+                            op1=ALU.max,
+                        )
+                    else:
+                        nc.scalar.activation(
+                            out=steep[:, k, :],
+                            in_=product[:, k, :],
+                            func=ACT.Relu,
+                            bias=bias_steep[:, c_tile : c_tile + 1],
+                            scale=1.0 - SLOPE,
+                        )
+                leaky_pieces[j].append((steep,) if one_piece else (steep, flat))
+
+        def join_pieces(j):
+            for bank in range(PRODUCT_BANKS):
+                steep, flat = leaky_pieces[j][bank]
+                nc.vector.tensor_tensor(out=steep[:], in0=steep[:], in1=flat[:], op=ALU.add)
+                leaky_pieces[j][bank] = (steep,)
 
         def add_up(j):
             for c_tile in range(C_TILES):
                 bank, k = divmod(c_tile, TILES_A_BANK)
                 half, quarter = divmod(c_tile, QUAD)
-                steep, flat = leaky_pieces[j][bank]
+                tiles = leaky_pieces[j][bank]
                 for r in range(ROW_TILES):
                     target = sums[(r, half)][:, quarter * P : (quarter + 1) * P]
                     pair_cols = slice(r * P, (r + 1) * P)
-                    nc.tensor.matmul(
-                        out=target,
-                        lhsT=steep[:, k, pair_cols],
-                        rhs=identity[:],
-                        is_transpose=True,
-                        start=(j == 0 and quarter == 0),
-                        stop=False,
-                    )
-                    nc.tensor.matmul(
-                        out=target,
-                        lhsT=flat[:, k, pair_cols],
-                        rhs=identity[:],
-                        is_transpose=True,
-                        start=False,
-                        stop=(j == NODES - 1 and quarter == QUAD - 1),
-                    )
+                    for n, piece in enumerate(tiles):
+                        nc.tensor.matmul(
+                            out=target,
+                            lhsT=piece[:, k, pair_cols],
+                            rhs=identity[:],
+                            is_transpose=True,
+                            start=(j == 0 and quarter == 0 and n == 0),
+                            stop=(j == NODES - 1 and quarter == QUAD - 1 and n == len(tiles) - 1),
+                        )
 
         units = NODES * PASSES
-        for unit in range(units + 1):
+        for unit in range(1, units + 1):
             if unit < units:
                 add_pairs(unit)
-            if unit > 0:
-                quantise(unit - 1)
+            quantise(unit - 1)
             if unit < units:
                 leaky_and_round(unit)
-            if unit > 0 and unit % PASSES == 0:
+            if unit % PASSES == 0:
                 j = unit // PASSES - 1
-                multiply(j)
+                if j == NODES - 1:
+                    join_pieces(j - 1)
+                multiply(j, one_piece=(j == NODES - 1))
                 if j > 0:
                     add_up(j - 1)
         add_up(NODES - 1)

@@ -29,6 +29,8 @@ QUAD = BANK // P
 TILES_A_BANK = BANK // ROWS
 PRODUCT_BANKS = C_TILES // TILES_A_BANK
 SLOPE = 0.2
+WARM_BEFORE_F = 4
+WARM_BEHIND_F = 4
 
 FLOPS = 2 * ROWS * (2 * C) * C + 2 * ROWS * NODES * C * C
 
@@ -39,6 +41,9 @@ def tile_nonlocalmp_pa_kernel(tc, F, W1_words, W1_scales, b1, W2_words, W2_scale
         ctx.enter_context(tc.manual_schedule())
         keep = ctx.enter_context(tc.tile_pool(name="keep", bufs=1))
         stage = ctx.enter_context(tc.tile_pool(name="stage", bufs=2))
+
+        zeros = keep.tile([P, BANK], BF16)
+        nc.gpsimd.memset(zeros[:], 0.0)
 
         w1_planes = keep.tile([P, C], U8, align_bytes=64)
         w2_planes = keep.tile([P, C], U8, align_bytes=64)
@@ -120,6 +125,13 @@ def tile_nonlocalmp_pa_kernel(tc, F, W1_words, W1_scales, b1, W2_words, W2_scale
 
         with tc.psum_pool(name="first_layer_banks", bufs=8) as banks:
             f_words = f_rows[:].bitcast(F32)
+            unread = banks.tile([P, BANK], F32, tag="bank")
+
+            def keep_warm(matmuls):
+                for n in range(matmuls):
+                    nc.tensor.matmul(out=unread[:], lhsT=zeros[:, 0:P], rhs=zeros[:], start=True, stop=True)
+
+            keep_warm(WARM_BEFORE_F)
             f_codes = keep.tile([P, PASSES, ROWS], U32, align_bytes=64)
             f_planes = keep.tile([P, PASSES, ROWS], U8, align_bytes=64)
             f_grouped = []
@@ -136,6 +148,7 @@ def tile_nonlocalmp_pa_kernel(tc, F, W1_words, W1_scales, b1, W2_words, W2_scale
                     in_=turned[:].rearrange("p r u n -> p r n u"),
                 )
                 f_grouped.append(grouped)
+            keep_warm(WARM_BEHIND_F)
             for g in range(PASSES):
                 nc.vector.quantize_mx(
                     out=f_codes[:, g, :].bitcast(FP8X4), scales=f_planes[:, g, :], in_=f_grouped[g][:]
@@ -146,7 +159,7 @@ def tile_nonlocalmp_pa_kernel(tc, F, W1_words, W1_scales, b1, W2_words, W2_scale
 
             for half in range(HALVES):
                 cols = slice(half * BANK, (half + 1) * BANK)
-                pieces_of_half = [(part, r) for part in range(2) for r in range(ROW_TILES)]
+                pieces_of_half = [(part, r) for part in (1, 0) for r in range(ROW_TILES)]
                 sorted_rows = {}
                 for part, r in pieces_of_half:
                     m_cols = slice(r * P, (r + 1) * P)
@@ -163,7 +176,7 @@ def tile_nonlocalmp_pa_kernel(tc, F, W1_words, W1_scales, b1, W2_words, W2_scale
                             stop=(g == PASSES - 1),
                         )
                     by_t = stage.tile([P, PACK, P], F32, name="by_t", bufs=2 * len(pieces_of_half))
-                    if part == 0 or half == 1:
+                    if r == 1 or half == 1:
                         nc.scalar.copy(out=by_t[:], in_=product[:].rearrange("r (p t) -> r t p", t=PACK))
                     else:
                         nc.vector.tensor_copy(out=by_t[:], in_=product[:].rearrange("r (p t) -> r t p", t=PACK))
@@ -208,6 +221,10 @@ def tile_nonlocalmp_pa_kernel(tc, F, W1_words, W1_scales, b1, W2_words, W2_scale
 
         out_rows = out.flatten_outer_dims()
         leaky_pieces = {}
+
+        all_banks = list(range(PRODUCT_BANKS))
+        early_banks = all_banks[: PRODUCT_BANKS // 2]
+        late_banks = all_banks[PRODUCT_BANKS // 2 :]
 
         def multiply(j, one_piece):
             codes, planes = h_words[j]
@@ -260,13 +277,13 @@ def tile_nonlocalmp_pa_kernel(tc, F, W1_words, W1_scales, b1, W2_words, W2_scale
                 leaky_pieces[j].append((steep,) if one_piece else (steep, flat))
 
         def join_pieces(j):
-            for bank in range(PRODUCT_BANKS):
+            for bank in all_banks:
                 steep, flat = leaky_pieces[j][bank]
                 nc.vector.tensor_tensor(out=steep[:], in0=steep[:], in1=flat[:], op=ALU.add)
                 leaky_pieces[j][bank] = (steep,)
 
-        def add_up(j):
-            for c_tile in range(C_TILES):
+        def add_up(j, banks):
+            for c_tile in range(banks[0] * TILES_A_BANK, (banks[-1] + 1) * TILES_A_BANK):
                 bank, k = divmod(c_tile, TILES_A_BANK)
                 half, quarter = divmod(c_tile, QUAD)
                 tiles = leaky_pieces[j][bank]
@@ -284,6 +301,7 @@ def tile_nonlocalmp_pa_kernel(tc, F, W1_words, W1_scales, b1, W2_words, W2_scale
                         )
 
         units = NODES * PASSES
+        joined = NODES - 2
         for unit in range(1, units + 1):
             if unit < units:
                 add_pairs(unit)
@@ -296,8 +314,10 @@ def tile_nonlocalmp_pa_kernel(tc, F, W1_words, W1_scales, b1, W2_words, W2_scale
                     join_pieces(j - 1)
                 multiply(j, one_piece=(j == NODES - 1))
                 if j > 0:
-                    add_up(j - 1)
-        add_up(NODES - 1)
+                    add_up(j - 1, late_banks if j - 1 < joined else all_banks)
+                if j < joined:
+                    add_up(j, early_banks)
+        add_up(NODES - 1, all_banks)
 
         for half in range(HALVES):
             for r in range(ROW_TILES):

@@ -30,7 +30,7 @@ TILES_A_BANK = BANK // ROWS
 PRODUCT_BANKS = C_TILES // TILES_A_BANK
 SLOPE = 0.2
 WARM_BEFORE_F = 4
-WARM_BEHIND_F = 4
+WARM_BEHIND_F = 2
 
 FLOPS = 2 * ROWS * (2 * C) * C + 2 * ROWS * NODES * C * C
 
@@ -67,7 +67,9 @@ def tile_nonlocalmp_pa_kernel(tc, F, W1_words, W1_scales, b1, W2_words, W2_scale
         w1_source = W1_words.rearrange("g p n t -> p g (n t)").bitcast(I32)
         for half in range(HALVES):
             cols = slice(half * BANK, (half + 1) * BANK)
-            nc.sync.dma_start(out=w1_words[:, :, cols].bitcast(I32), in_=w1_source[:, :, cols])
+            for part in (1, 0):
+                of_part = slice(PASSES * part, PASSES * (part + 1))
+                nc.sync.dma_start(out=w1_words[:, of_part, cols].bitcast(I32), in_=w1_source[:, of_part, cols])
 
         b1_t = keep.tile([P, PASSES, PACK], BF16)
         nc.scalar.dma_start(out=b1_t[:], in_=b1.rearrange("(g p t) -> p g t", p=P, t=PACK))
@@ -143,7 +145,8 @@ def tile_nonlocalmp_pa_kernel(tc, F, W1_words, W1_scales, b1, W2_words, W2_scale
                             turned[:, r, u, :], f_words[:, r, 256 * g + u : 256 * (g + 1) : 2], identity[:]
                         )
                 grouped = stage.tile([P, ROWS * PACK], BF16, name="f_grouped", align_bytes=64)
-                nc.vector.tensor_copy(
+                copy_words = nc.vector.tensor_copy if g == 0 else nc.scalar.copy
+                copy_words(
                     out=grouped[:].bitcast(F32).rearrange("p (r n u) -> p r n u", r=ROW_TILES, u=2),
                     in_=turned[:].rearrange("p r u n -> p r n u"),
                 )
@@ -317,7 +320,19 @@ def tile_nonlocalmp_pa_kernel(tc, F, W1_words, W1_scales, b1, W2_words, W2_scale
                     add_up(j - 1, late_banks if j - 1 < joined else all_banks)
                 if j < joined:
                     add_up(j, early_banks)
-        add_up(NODES - 1, all_banks)
+        for half in range(HALVES):
+            for r in range(ROW_TILES):
+                for quarter in range(QUAD):
+                    bank, k = divmod(half * QUAD + quarter, TILES_A_BANK)
+                    (piece,) = leaky_pieces[NODES - 1][bank]
+                    nc.tensor.matmul(
+                        out=sums[(r, half)][:, quarter * P : (quarter + 1) * P],
+                        lhsT=piece[:, k, r * P : (r + 1) * P],
+                        rhs=identity[:],
+                        is_transpose=True,
+                        start=False,
+                        stop=(quarter == QUAD - 1),
+                    )
 
         for half in range(HALVES):
             for r in range(ROW_TILES):

@@ -134,27 +134,29 @@ def tile_nonlocalmp_pa_kernel(tc, F, W1_words, W1_scales, b1, W2_words, W2_scale
                     nc.tensor.matmul(out=unread[:], lhsT=zeros[:, 0:P], rhs=zeros[:], start=True, stop=True)
 
             keep_warm(WARM_BEFORE_F)
-            f_codes = keep.tile([P, PASSES, ROWS], U32, align_bytes=64)
-            f_planes = keep.tile([P, PASSES, ROWS], U8, align_bytes=64)
+            f_codes = keep.tile([P, ROW_TILES, PASSES, P], U32, align_bytes=64)
+            f_planes = keep.tile([P, ROW_TILES, PASSES, P], U8, align_bytes=64)
             f_grouped = []
-            for g in range(PASSES):
-                turned = banks.tile([P, ROW_TILES, 2, P], F32, tag="bank")
-                for r in range(ROW_TILES):
+            for r in range(ROW_TILES):
+                turned = banks.tile([P, PASSES, 2, P], F32, tag="bank")
+                for g in range(PASSES):
                     for u in range(2):
                         nc.tensor.transpose(
-                            turned[:, r, u, :], f_words[:, r, 256 * g + u : 256 * (g + 1) : 2], identity[:]
+                            turned[:, g, u, :], f_words[:, r, 256 * g + u : 256 * (g + 1) : 2], identity[:]
                         )
                 grouped = stage.tile([P, ROWS * PACK], BF16, name="f_grouped", align_bytes=64)
-                copy_words = nc.vector.tensor_copy if g == 0 else nc.scalar.copy
+                copy_words = nc.vector.tensor_copy if r == 0 else nc.scalar.copy
                 copy_words(
-                    out=grouped[:].bitcast(F32).rearrange("p (r n u) -> p r n u", r=ROW_TILES, u=2),
-                    in_=turned[:].rearrange("p r u n -> p r n u"),
+                    out=grouped[:].bitcast(F32).rearrange("p (g n u) -> p g n u", g=PASSES, u=2),
+                    in_=turned[:].rearrange("p g u n -> p g n u"),
                 )
                 f_grouped.append(grouped)
             keep_warm(WARM_BEHIND_F)
-            for g in range(PASSES):
+            for r in range(ROW_TILES):
                 nc.vector.quantize_mx(
-                    out=f_codes[:, g, :].bitcast(FP8X4), scales=f_planes[:, g, :], in_=f_grouped[g][:]
+                    out=f_codes[:, r].rearrange("p g n -> p (g n)").bitcast(FP8X4),
+                    scales=f_planes[:, r].rearrange("p g n -> p (g n)"),
+                    in_=f_grouped[r][:],
                 )
             b2_wide = keep.tile([P, P], F32)
             nc.scalar.copy(out=b2_wide[:], in_=b2_rows[:])
@@ -165,14 +167,13 @@ def tile_nonlocalmp_pa_kernel(tc, F, W1_words, W1_scales, b1, W2_words, W2_scale
                 pieces_of_half = [(part, r) for part in (1, 0) for r in range(ROW_TILES)]
                 sorted_rows = {}
                 for part, r in pieces_of_half:
-                    m_cols = slice(r * P, (r + 1) * P)
                     product = banks.tile([P, BANK], F32, tag="bank")
                     for g in range(PASSES):
                         w1_pass = PASSES * part + g
                         nc.tensor.matmul_mx(
                             out=product[:],
-                            lhsT=f_codes[:, g, m_cols].bitcast(FP8X4),
-                            lhsT_scale=f_planes[:, g, m_cols],
+                            lhsT=f_codes[:, r, g, :].bitcast(FP8X4),
+                            lhsT_scale=f_planes[:, r, g, :],
                             rhs=w1_words[:, w1_pass, cols].bitcast(FP8X4),
                             rhs_scale=w1_planes[4 * w1_pass : P, cols],
                             start=(g == 0),

@@ -22,11 +22,16 @@ NODES = 16
 C = 1024
 ROWS = SETS * NODES
 ROW_TILES = ROWS // P
+TILE_SETS = P // NODES
 PASSES = C // K_PASS
 HALVES = C // BANK
 C_TILES = C // P
 QUAD = BANK // P
-TILES_A_BANK = BANK // ROWS
+J_STEP = 2
+PAIRS = J_STEP * P
+STEPS_A_TILE = NODES // J_STEP
+STEPS = ROW_TILES * STEPS_A_TILE
+TILES_A_BANK = BANK // PAIRS
 PRODUCT_BANKS = C_TILES // TILES_A_BANK
 SLOPE = 0.2
 WARM_BEFORE_F = 4
@@ -71,8 +76,11 @@ def tile_nonlocalmp_pa_kernel(tc, F, W1_words, W1_scales, b1, W2_words, W2_scale
                 of_part = slice(PASSES * part, PASSES * (part + 1))
                 nc.sync.dma_start(out=w1_words[:, of_part, cols].bitcast(I32), in_=w1_source[:, of_part, cols])
 
-        b1_t = keep.tile([P, PASSES, PACK], BF16)
-        nc.scalar.dma_start(out=b1_t[:], in_=b1.rearrange("(g p t) -> p g t", p=P, t=PACK))
+        b1_row = keep.tile([P, C], BF16)
+        nc.vector.memset(b1_row[:], 0.0)
+        nc.scalar.dma_start(out=b1_row[0:1, :], in_=b1.rearrange("(o c) -> o c", o=1))
+        ones = keep.tile([P, P], BF16)
+        nc.gpsimd.memset(ones[:], 1.0)
         b2_rows = keep.tile([P, P], BF16)
         nc.vector.memset(b2_rows[:], 0.0)
         nc.scalar.dma_start(out=b2_rows[0:C_TILES, :], in_=b2.rearrange("(c p) -> c p", p=P))
@@ -84,144 +92,189 @@ def tile_nonlocalmp_pa_kernel(tc, F, W1_words, W1_scales, b1, W2_words, W2_scale
         identity = keep.tile([P, P], F32)
         make_identity(nc, identity[:])
 
-        a_t = keep.tile([P, PASSES, SETS, NODES, PACK], F32)
-        b_t = keep.tile([P, PASSES, SETS, NODES, PACK], F32)
+        b_t = keep.tile([P, ROW_TILES, PASSES, NODES, TILE_SETS, PACK], F32)
         bias_steep = keep.tile([P, C_TILES], F32)
         bias_flat = keep.tile([P, C_TILES], F32)
         bias_whole = keep.tile([P, C_TILES], F32)
 
-
         hidden = ctx.enter_context(tc.tile_pool(name="hidden", bufs=2))
         words = ctx.enter_context(tc.tile_pool(name="words", bufs=4))
+        pieces = ctx.enter_context(tc.tile_pool(name="pieces", bufs=2 * PRODUCT_BANKS))
+        results = ctx.enter_context(tc.tile_pool(name="results", bufs=ROW_TILES * HALVES))
+
+        banks = ctx.enter_context(tc.psum_pool(name="banks", bufs=PRODUCT_BANKS))
+        a_banks = ctx.enter_context(tc.psum_pool(name="a_banks", bufs=1))
+        sum_banks = ctx.enter_context(tc.psum_pool(name="sum_banks", bufs=1))
+
+        a_t = {}
+        sums = {}
+
+        def open_sum(r, half):
+            sums[(r, half)] = sum_banks.tile([P, BANK], F32, name="sum_%d" % half)
+
         h_sum = {}
         h_rounded = {}
         h_words = {}
 
-        def add_pairs(unit):
-            j, g = divmod(unit, PASSES)
-            total = hidden.tile([P, SETS, NODES, PACK], F32, name="h_sum")
+        def add_pairs(unit, first=0, last=J_STEP):
+            step, g = unit
+            r, of_tile = divmod(step, STEPS_A_TILE)
+            if first == 0:
+                total = hidden.tile([P, J_STEP, TILE_SETS, NODES, PACK], F32, name="h_sum")
+                h_sum[unit] = total
+            a_view = a_t[(r, g)][:].rearrange("p t (b i) -> p b i t", b=TILE_SETS)
+            b_view = b_t[:, r, g, of_tile * J_STEP + first : of_tile * J_STEP + last]
+            shape = [P, last - first, TILE_SETS, NODES, PACK]
             nc.vector.tensor_tensor(
-                out=total[:],
-                in0=a_t[:, g],
-                in1=b_t[:, g, :, j, :].unsqueeze(2).to_broadcast([P, SETS, NODES, PACK]),
+                out=h_sum[unit][:, first:last],
+                in0=a_view.unsqueeze(1).to_broadcast(shape),
+                in1=b_view.unsqueeze(3).to_broadcast(shape),
                 op=ALU.add,
             )
-            h_sum[unit] = total
 
         def leaky_and_round(unit):
-            total = h_sum[unit][:].rearrange("p b n t -> p (b n t)")
-            rounded = hidden.tile([P, ROWS * PACK], BF16, name="h_rounded", align_bytes=64)
+            total = h_sum[unit][:].rearrange("p j b n t -> p (j b n t)")
+            rounded = hidden.tile([P, PAIRS * PACK], BF16, name="h_rounded", align_bytes=64)
             nc.vector.scalar_tensor_tensor(
                 out=rounded[:], in0=total, scalar=SLOPE, in1=total, op0=ALU.mult, op1=ALU.max
             )
             h_rounded[unit] = rounded
 
         def quantise(unit):
-            j, g = divmod(unit, PASSES)
-            if g == 0:
-                codes = words.tile([P, PASSES, ROWS], U32, name="h_codes", align_bytes=64)
-                planes = words.tile([P, PASSES, ROWS], U8, name="h_planes", align_bytes=64)
-                h_words[j] = (codes, planes)
-            codes, planes = h_words[j]
+            step, g = unit
+            if step not in h_words:
+                codes = words.tile([P, PASSES, PAIRS], U32, name="h_codes", align_bytes=64)
+                planes = words.tile([P, PASSES, PAIRS], U8, name="h_planes", align_bytes=64)
+                h_words[step] = (codes, planes)
+            codes, planes = h_words[step]
             nc.vector.quantize_mx(out=codes[:, g, :].bitcast(FP8X4), scales=planes[:, g, :], in_=h_rounded[unit][:])
 
-        with tc.psum_pool(name="first_layer_banks", bufs=8) as banks:
-            f_words = f_rows[:].bitcast(F32)
-            unread = banks.tile([P, BANK], F32, tag="bank")
+        f_words = f_rows[:].bitcast(F32)
+        unread = sum_banks.tile([P, BANK], F32, name="sum_0")
 
-            def keep_warm(matmuls):
-                for n in range(matmuls):
-                    nc.tensor.matmul(out=unread[:], lhsT=zeros[:, 0:P], rhs=zeros[:], start=True, stop=True)
+        def keep_warm(matmuls):
+            for n in range(matmuls):
+                nc.tensor.matmul(out=unread[:], lhsT=zeros[:, 0:P], rhs=zeros[:], start=True, stop=True)
 
-            keep_warm(WARM_BEFORE_F)
-            f_codes = keep.tile([P, ROW_TILES, PASSES, P], U32, align_bytes=64)
-            f_planes = keep.tile([P, ROW_TILES, PASSES, P], U8, align_bytes=64)
-            f_grouped = []
-            for r in range(ROW_TILES):
-                turned = banks.tile([P, PASSES, 2, P], F32, tag="bank")
-                for g in range(PASSES):
-                    for u in range(2):
-                        nc.tensor.transpose(
-                            turned[:, g, u, :], f_words[:, r, 256 * g + u : 256 * (g + 1) : 2], identity[:]
-                        )
-                grouped = stage.tile([P, ROWS * PACK], BF16, name="f_grouped", align_bytes=64)
-                copy_words = nc.vector.tensor_copy if r == 0 else nc.scalar.copy
-                copy_words(
-                    out=grouped[:].bitcast(F32).rearrange("p (g n u) -> p g n u", g=PASSES, u=2),
-                    in_=turned[:].rearrange("p g u n -> p g n u"),
-                )
-                f_grouped.append(grouped)
-            keep_warm(WARM_BEHIND_F)
-            for r in range(ROW_TILES):
-                nc.vector.quantize_mx(
-                    out=f_codes[:, r].rearrange("p g n -> p (g n)").bitcast(FP8X4),
-                    scales=f_planes[:, r].rearrange("p g n -> p (g n)"),
-                    in_=f_grouped[r][:],
-                )
-            b2_wide = keep.tile([P, P], F32)
-            nc.scalar.copy(out=b2_wide[:], in_=b2_rows[:])
-
-
-            for half in range(HALVES):
-                cols = slice(half * BANK, (half + 1) * BANK)
-                pieces_of_half = [(part, r) for part in (1, 0) for r in range(ROW_TILES)]
-                sorted_rows = {}
-                for part, r in pieces_of_half:
-                    product = banks.tile([P, BANK], F32, tag="bank")
-                    for g in range(PASSES):
-                        w1_pass = PASSES * part + g
-                        nc.tensor.matmul_mx(
-                            out=product[:],
-                            lhsT=f_codes[:, r, g, :].bitcast(FP8X4),
-                            lhsT_scale=f_planes[:, r, g, :],
-                            rhs=w1_words[:, w1_pass, cols].bitcast(FP8X4),
-                            rhs_scale=w1_planes[4 * w1_pass : P, cols],
-                            start=(g == 0),
-                            stop=(g == PASSES - 1),
-                        )
-                    by_t = stage.tile([P, PACK, P], F32, name="by_t", bufs=2 * len(pieces_of_half))
-                    if r == 1 or half == 1:
-                        nc.scalar.copy(out=by_t[:], in_=product[:].rearrange("r (p t) -> r t p", t=PACK))
-                    else:
-                        nc.vector.tensor_copy(out=by_t[:], in_=product[:].rearrange("r (p t) -> r t p", t=PACK))
-                    sorted_rows[(part, r)] = by_t
-
-                for part, r in pieces_of_half:
-                    turned = banks.tile([P, PACK, P], F32, tag="bank")
-                    for t in range(PACK):
-                        nc.tensor.transpose(turned[:, t, :], sorted_rows[(part, r)][:, t, :], identity[:])
-                    sets = slice(r * P // NODES, (r + 1) * P // NODES)
-                    if part == 0:
-                        nc.scalar.copy(
-                            out=a_t[:, half, sets, :, :].rearrange("p b n t -> p (b n) t"),
-                            in_=turned[:].rearrange("p t n -> p n t"),
-                        )
-                    else:
-                        nc.vector.tensor_tensor(
-                            out=b_t[:, half, sets, :, :].rearrange("p b n t -> p (b n) t"),
-                            in0=turned[:].rearrange("p t n -> p n t"),
-                            in1=b1_t[:, half, :].unsqueeze(1).to_broadcast([P, P, PACK]),
-                            op=ALU.add,
-                        )
-                if half == 0:
-                    add_pairs(0)
-                    leaky_and_round(0)
-
-            b2_turned = banks.tile([P, P], F32, tag="bank")
-            nc.tensor.transpose(b2_turned[:], b2_wide[:], identity[:])
-            nc.scalar.mul(out=bias_steep[:], in_=b2_turned[:, 0:C_TILES], mul=1.0 - SLOPE)
-            nc.scalar.mul(out=bias_flat[:], in_=b2_turned[:, 0:C_TILES], mul=SLOPE)
-            nc.scalar.copy(out=bias_whole[:], in_=b2_turned[:, 0:C_TILES])
-
-        pieces = ctx.enter_context(tc.tile_pool(name="pieces", bufs=2 * PRODUCT_BANKS))
-        results = ctx.enter_context(tc.tile_pool(name="results", bufs=ROW_TILES * HALVES))
-        product_banks = ctx.enter_context(tc.psum_pool(name="product_banks", bufs=PRODUCT_BANKS))
-        sum_banks = ctx.enter_context(tc.psum_pool(name="sum_banks", bufs=1))
-
-        sums = {}
+        keep_warm(WARM_BEFORE_F)
+        f_codes = keep.tile([P, ROW_TILES, PASSES, P], U32, align_bytes=64)
+        f_planes = keep.tile([P, ROW_TILES, PASSES, P], U8, align_bytes=64)
+        f_grouped = []
         for r in range(ROW_TILES):
+            turned = banks.tile([P, PASSES, 2, P], F32, tag="bank")
+            for g in range(PASSES):
+                for u in range(2):
+                    nc.tensor.transpose(
+                        turned[:, g, u, :], f_words[:, r, 256 * g + u : 256 * (g + 1) : 2], identity[:]
+                    )
+            grouped = stage.tile([P, ROWS * PACK], BF16, name="f_grouped", align_bytes=64)
+            copy_words = nc.vector.tensor_copy if r == 0 else nc.scalar.copy
+            copy_words(
+                out=grouped[:].bitcast(F32).rearrange("p (g n u) -> p g n u", g=PASSES, u=2),
+                in_=turned[:].rearrange("p g u n -> p g n u"),
+            )
+            f_grouped.append(grouped)
+        keep_warm(WARM_BEHIND_F)
+        for r in range(ROW_TILES):
+            nc.vector.quantize_mx(
+                out=f_codes[:, r].rearrange("p g n -> p (g n)").bitcast(FP8X4),
+                scales=f_planes[:, r].rearrange("p g n -> p (g n)"),
+                in_=f_grouped[r][:],
+            )
+        b2_wide = keep.tile([P, P], F32)
+        nc.scalar.copy(out=b2_wide[:], in_=b2_rows[:])
+
+        sorted_rows = {}
+
+        def first_layer(part, r, half, on_vector):
+            cols = slice(half * BANK, (half + 1) * BANK)
+            product = banks.tile([P, BANK], F32, tag="bank")
+            for g in range(PASSES):
+                w1_pass = PASSES * part + g
+                nc.tensor.matmul_mx(
+                    out=product[:],
+                    lhsT=f_codes[:, r, g, :].bitcast(FP8X4),
+                    lhsT_scale=f_planes[:, r, g, :],
+                    rhs=w1_words[:, w1_pass, cols].bitcast(FP8X4),
+                    rhs_scale=w1_planes[4 * w1_pass : P, cols],
+                    start=(g == 0),
+                    stop=(g == PASSES - 1),
+                )
+            by_t = keep.tile([P, PACK, P], F32, name="by_t_%d%d%d" % (part, r, half))
+            copy_rows = nc.vector.tensor_copy if on_vector else nc.scalar.copy
+            copy_rows(out=by_t[:], in_=product[:].rearrange("r (p t) -> r t p", t=PACK))
+            sorted_rows[(part, r, half)] = by_t
+
+        def turn_a(r, half):
+            a_t[(r, half)] = a_banks.tile([P, PACK, P], F32, name="a_%d" % half)
+            for t in range(PACK):
+                nc.tensor.transpose(a_t[(r, half)][:, t, :], sorted_rows[(0, r, half)][:, t, :], identity[:])
+
+        b_turned = {}
+
+        def turn_b(r, half):
+            if r == 0:
+                turned = banks.tile([P, PACK, P], F32, tag="bank")
+            else:
+                turned = sum_banks.tile([P, PACK, P], F32, name="sum_%d" % half)
+            for t in range(PACK):
+                nc.tensor.matmul(
+                    out=turned[:, t, :],
+                    lhsT=b1_row[:, half * BANK + t : (half + 1) * BANK : PACK],
+                    rhs=ones[:],
+                    start=(t == 0),
+                    stop=False,
+                )
+            for t in range(PACK):
+                nc.tensor.matmul(
+                    out=turned[:, t, :],
+                    lhsT=sorted_rows[(1, r, half)][:, t, :],
+                    rhs=identity[:],
+                    is_transpose=True,
+                    start=False,
+                    stop=(t == PACK - 1),
+                )
+            b_turned[(r, half)] = turned
+
+        def copy_b(r, half, copy):
+            copy(
+                out=b_t[:, r, half].rearrange("p j b t -> p b j t"),
+                in_=b_turned[(r, half)][:].rearrange("p t (b j) -> p b j t", b=TILE_SETS),
+            )
+
+        units = [(step, g) for step in range(STEPS) for g in range(PASSES)]
+
+        first_layer(1, 0, 0, on_vector=True)
+        first_layer(0, 0, 0, on_vector=False)
+        turn_b(0, 0)
+        turn_a(0, 0)
+        copy_b(0, 0, nc.vector.tensor_copy)
+        add_pairs(units[0])
+        leaky_and_round(units[0])
+        first_layer(1, 0, 1, on_vector=False)
+        first_layer(0, 0, 1, on_vector=False)
+        turn_b(0, 1)
+        turn_a(0, 1)
+        copy_b(0, 1, nc.scalar.copy)
+        add_pairs(units[1])
+        quantise(units[0])
+        leaky_and_round(units[1])
+        for part in (1, 0):
             for half in range(HALVES):
-                sums[(r, half)] = sum_banks.tile([P, BANK], F32, name="sum_%d_%d" % (r, half))
+                first_layer(part, 1, half, on_vector=False)
+        for half in range(HALVES):
+            turn_b(1, half)
+            copy_b(1, half, nc.scalar.copy)
+        add_pairs(units[2], 0, 1)
+        quantise(units[1])
+        add_pairs(units[2], 1, J_STEP)
+        leaky_and_round(units[2])
+
+        b2_turned = banks.tile([P, P], F32, tag="bank")
+        nc.tensor.transpose(b2_turned[:], b2_wide[:], identity[:])
+        nc.scalar.mul(out=bias_steep[:], in_=b2_turned[:, 0:C_TILES], mul=1.0 - SLOPE)
+        nc.scalar.mul(out=bias_flat[:], in_=b2_turned[:, 0:C_TILES], mul=SLOPE)
+        nc.scalar.copy(out=bias_whole[:], in_=b2_turned[:, 0:C_TILES])
 
         out_rows = out.flatten_outer_dims()
         leaky_pieces = {}
@@ -230,13 +283,13 @@ def tile_nonlocalmp_pa_kernel(tc, F, W1_words, W1_scales, b1, W2_words, W2_scale
         early_banks = all_banks[: PRODUCT_BANKS // 2]
         late_banks = all_banks[PRODUCT_BANKS // 2 :]
 
-        def multiply(j, one_piece):
-            codes, planes = h_words[j]
-            leaky_pieces[j] = []
+        def multiply(step, one_piece):
+            codes, planes = h_words[step]
+            leaky_pieces[step] = []
             for bank in range(PRODUCT_BANKS):
-                product = product_banks.tile([P, TILES_A_BANK, ROWS], F32, name="product")
-                steep = pieces.tile([P, TILES_A_BANK, ROWS], F32, name="steep")
-                flat = pieces.tile([P, TILES_A_BANK, ROWS], F32, name="flat")
+                product = banks.tile([P, TILES_A_BANK, PAIRS], F32, tag="bank")
+                steep = pieces.tile([P, TILES_A_BANK, PAIRS], F32, name="steep")
+                flat = pieces.tile([P, TILES_A_BANK, PAIRS], F32, name="flat")
                 for k in range(TILES_A_BANK):
                     c_tile = bank * TILES_A_BANK + k
                     m_cols = slice(c_tile * P, (c_tile + 1) * P)
@@ -278,68 +331,85 @@ def tile_nonlocalmp_pa_kernel(tc, F, W1_words, W1_scales, b1, W2_words, W2_scale
                             bias=bias_steep[:, c_tile : c_tile + 1],
                             scale=1.0 - SLOPE,
                         )
-                leaky_pieces[j].append((steep,) if one_piece else (steep, flat))
+                leaky_pieces[step].append((steep,) if one_piece else (steep, flat))
 
-        def join_pieces(j):
+        def join_pieces(step):
             for bank in all_banks:
-                steep, flat = leaky_pieces[j][bank]
+                steep, flat = leaky_pieces[step][bank]
                 nc.vector.tensor_tensor(out=steep[:], in0=steep[:], in1=flat[:], op=ALU.add)
-                leaky_pieces[j][bank] = (steep,)
+                leaky_pieces[step][bank] = (steep,)
 
-        def add_up(j, banks):
-            for c_tile in range(banks[0] * TILES_A_BANK, (banks[-1] + 1) * TILES_A_BANK):
+        def add_up(step, some_banks):
+            r, of_tile = divmod(step, STEPS_A_TILE)
+            for c_tile in range(some_banks[0] * TILES_A_BANK, (some_banks[-1] + 1) * TILES_A_BANK):
                 bank, k = divmod(c_tile, TILES_A_BANK)
                 half, quarter = divmod(c_tile, QUAD)
-                tiles = leaky_pieces[j][bank]
-                for r in range(ROW_TILES):
-                    target = sums[(r, half)][:, quarter * P : (quarter + 1) * P]
-                    pair_cols = slice(r * P, (r + 1) * P)
-                    for n, piece in enumerate(tiles):
-                        nc.tensor.matmul(
-                            out=target,
-                            lhsT=piece[:, k, pair_cols],
-                            rhs=identity[:],
-                            is_transpose=True,
-                            start=(j == 0 and quarter == 0 and n == 0),
-                            stop=(j == NODES - 1 and quarter == QUAD - 1 and n == len(tiles) - 1),
-                        )
-
-        units = NODES * PASSES
-        joined = NODES - 2
-        for unit in range(1, units + 1):
-            if unit < units:
-                add_pairs(unit)
-            quantise(unit - 1)
-            if unit < units:
-                leaky_and_round(unit)
-            if unit % PASSES == 0:
-                j = unit // PASSES - 1
-                if j == NODES - 1:
-                    join_pieces(j - 1)
-                multiply(j, one_piece=(j == NODES - 1))
-                if j > 0:
-                    add_up(j - 1, late_banks if j - 1 < joined else all_banks)
-                if j < joined:
-                    add_up(j, early_banks)
-        for half in range(HALVES):
-            for r in range(ROW_TILES):
-                for quarter in range(QUAD):
-                    bank, k = divmod(half * QUAD + quarter, TILES_A_BANK)
-                    (piece,) = leaky_pieces[NODES - 1][bank]
+                blocks = [(j, piece) for j in range(J_STEP) for piece in leaky_pieces[step][bank]]
+                for n, (j, piece) in enumerate(blocks):
                     nc.tensor.matmul(
                         out=sums[(r, half)][:, quarter * P : (quarter + 1) * P],
-                        lhsT=piece[:, k, r * P : (r + 1) * P],
+                        lhsT=piece[:, k, j * P : (j + 1) * P],
+                        rhs=identity[:],
+                        is_transpose=True,
+                        start=(of_tile == 0 and quarter == 0 and n == 0),
+                        stop=(of_tile == STEPS_A_TILE - 1 and quarter == QUAD - 1 and n == len(blocks) - 1),
+                    )
+
+        def store(r, half, copy):
+            result = results.tile([P, BANK], F32, name="result")
+            copy(out=result[:], in_=sums[(r, half)][:])
+            nc.sync.dma_start(out=out_rows[r * P : (r + 1) * P, half * BANK : (half + 1) * BANK], in_=result[:])
+
+        joined = STEPS - 2
+        tile_end = STEPS_A_TILE - 1
+
+        def sum_up(step):
+            if step > 0:
+                add_up(step - 1, late_banks if step - 1 < joined else all_banks)
+                if step - 1 == tile_end:
+                    store(0, 1, nc.scalar.copy)
+                    open_sum(1, 1)
+            if step < joined:
+                add_up(step, early_banks)
+                if step == tile_end:
+                    store(0, 0, nc.scalar.copy)
+                    open_sum(1, 0)
+
+        for half in range(HALVES):
+            open_sum(0, half)
+        multiply(0, one_piece=False)
+        sum_up(0)
+        for n in range(3, len(units) + 1):
+            if n < len(units):
+                add_pairs(units[n])
+            quantise(units[n - 1])
+            if n < len(units):
+                leaky_and_round(units[n])
+            if units[n - 1] == (tile_end, 0):
+                turn_a(1, 1)
+                sum_up(tile_end - 1)
+            if n % PASSES == 0:
+                step = n // PASSES - 1
+                if step == STEPS - 1:
+                    join_pieces(step - 1)
+                if step == tile_end - 1:
+                    turn_a(1, 0)
+                multiply(step, one_piece=(step == STEPS - 1))
+                if step != tile_end - 1:
+                    sum_up(step)
+        last = STEPS - 1
+        for half in range(HALVES):
+            for quarter in range(QUAD):
+                bank, k = divmod(half * QUAD + quarter, TILES_A_BANK)
+                (piece,) = leaky_pieces[last][bank]
+                for j in range(J_STEP):
+                    nc.tensor.matmul(
+                        out=sums[(1, half)][:, quarter * P : (quarter + 1) * P],
+                        lhsT=piece[:, k, j * P : (j + 1) * P],
                         rhs=identity[:],
                         is_transpose=True,
                         start=False,
-                        stop=(quarter == QUAD - 1),
+                        stop=(quarter == QUAD - 1 and j == J_STEP - 1),
                     )
-
         for half in range(HALVES):
-            for r in range(ROW_TILES):
-                result = results.tile([P, BANK], F32, name="result")
-                if r == 0:
-                    nc.vector.tensor_copy(out=result[:], in_=sums[(r, half)][:])
-                else:
-                    nc.scalar.copy(out=result[:], in_=sums[(r, half)][:])
-                nc.sync.dma_start(out=out_rows[r * P : (r + 1) * P, half * BANK : (half + 1) * BANK], in_=result[:])
+            store(1, half, nc.vector.tensor_copy if half == 0 else nc.scalar.copy)

@@ -291,7 +291,7 @@ def tile_nonlocalmp_pa_kernel(tc, F, W1_words, W1_scales, b1, W2_words, W2_scale
                 steep = pieces.tile([P, TILES_A_BANK, PAIRS], F32, name="steep")
                 flat = pieces.tile([P, TILES_A_BANK, PAIRS], F32, name="flat")
                 for k in range(TILES_A_BANK):
-                    c_tile = bank * TILES_A_BANK + k
+                    c_tile = bank + k * PRODUCT_BANKS
                     m_cols = slice(c_tile * P, (c_tile + 1) * P)
                     for g in range(PASSES):
                         nc.tensor.matmul_mx(
@@ -304,7 +304,7 @@ def tile_nonlocalmp_pa_kernel(tc, F, W1_words, W1_scales, b1, W2_words, W2_scale
                             stop=(g == PASSES - 1),
                         )
                 for k in range(TILES_A_BANK):
-                    c_tile = bank * TILES_A_BANK + k
+                    c_tile = bank + k * PRODUCT_BANKS
                     nc.scalar.activation(
                         out=flat[:, k, :],
                         in_=product[:, k, :],
@@ -313,7 +313,7 @@ def tile_nonlocalmp_pa_kernel(tc, F, W1_words, W1_scales, b1, W2_words, W2_scale
                         scale=SLOPE,
                     )
                 for k in range(TILES_A_BANK):
-                    c_tile = bank * TILES_A_BANK + k
+                    c_tile = bank + k * PRODUCT_BANKS
                     if one_piece:
                         nc.vector.scalar_tensor_tensor(
                             out=steep[:, k, :],
@@ -341,19 +341,24 @@ def tile_nonlocalmp_pa_kernel(tc, F, W1_words, W1_scales, b1, W2_words, W2_scale
 
         def add_up(step, some_banks):
             r, of_tile = divmod(step, STEPS_A_TILE)
-            for c_tile in range(some_banks[0] * TILES_A_BANK, (some_banks[-1] + 1) * TILES_A_BANK):
-                bank, k = divmod(c_tile, TILES_A_BANK)
-                half, quarter = divmod(c_tile, QUAD)
-                blocks = [(j, piece) for j in range(J_STEP) for piece in leaky_pieces[step][bank]]
-                for n, (j, piece) in enumerate(blocks):
-                    nc.tensor.matmul(
-                        out=sums[(r, half)][:, quarter * P : (quarter + 1) * P],
-                        lhsT=piece[:, k, j * P : (j + 1) * P],
-                        rhs=identity[:],
-                        is_transpose=True,
-                        start=(of_tile == 0 and quarter == 0 and n == 0),
-                        stop=(of_tile == STEPS_A_TILE - 1 and quarter == QUAD - 1 and n == len(blocks) - 1),
-                    )
+            for bank in some_banks:
+                pieces_here = leaky_pieces[step][bank]
+                for j in range(J_STEP):
+                    for half in range(HALVES):
+                        for n, piece in enumerate(pieces_here):
+                            nc.tensor.matmul(
+                                out=sums[(r, half)][:, bank * P : (bank + 1) * P],
+                                lhsT=piece[:, half, j * P : (j + 1) * P],
+                                rhs=identity[:],
+                                is_transpose=True,
+                                start=(of_tile == 0 and bank == 0 and j == 0 and n == 0),
+                                stop=(
+                                    of_tile == STEPS_A_TILE - 1
+                                    and bank == PRODUCT_BANKS - 1
+                                    and j == J_STEP - 1
+                                    and n == len(pieces_here) - 1
+                                ),
+                            )
 
         def store(r, half, copy):
             result = results.tile([P, BANK], F32, name="result")
@@ -365,15 +370,13 @@ def tile_nonlocalmp_pa_kernel(tc, F, W1_words, W1_scales, b1, W2_words, W2_scale
 
         def sum_up(step):
             if step > 0:
-                add_up(step - 1, late_banks if step - 1 < joined else all_banks)
+                add_up(step - 1, late_banks if step - 1 < joined and step - 1 != tile_end + 1 else all_banks)
                 if step - 1 == tile_end:
-                    store(0, 1, nc.scalar.copy)
-                    open_sum(1, 1)
-            if step < joined:
+                    for half in range(HALVES):
+                        store(0, half, nc.scalar.copy)
+                        open_sum(1, half)
+            if step < joined and step != tile_end + 1:
                 add_up(step, early_banks)
-                if step == tile_end:
-                    store(0, 0, nc.scalar.copy)
-                    open_sum(1, 0)
 
         for half in range(HALVES):
             open_sum(0, half)
@@ -399,17 +402,16 @@ def tile_nonlocalmp_pa_kernel(tc, F, W1_words, W1_scales, b1, W2_words, W2_scale
                     sum_up(step)
         last = STEPS - 1
         for half in range(HALVES):
-            for quarter in range(QUAD):
-                bank, k = divmod(half * QUAD + quarter, TILES_A_BANK)
+            for bank in all_banks:
                 (piece,) = leaky_pieces[last][bank]
                 for j in range(J_STEP):
                     nc.tensor.matmul(
-                        out=sums[(1, half)][:, quarter * P : (quarter + 1) * P],
-                        lhsT=piece[:, k, j * P : (j + 1) * P],
+                        out=sums[(1, half)][:, bank * P : (bank + 1) * P],
+                        lhsT=piece[:, half, j * P : (j + 1) * P],
                         rhs=identity[:],
                         is_transpose=True,
                         start=False,
-                        stop=(quarter == QUAD - 1 and j == J_STEP - 1),
+                        stop=(bank == PRODUCT_BANKS - 1 and j == J_STEP - 1),
                     )
         for half in range(HALVES):
             store(1, half, nc.vector.tensor_copy if half == 0 else nc.scalar.copy)

@@ -99,7 +99,7 @@ def tile_nonlocalmp_pa_kernel(tc, F, W1_words, W1_scales, b1, W2_words, W2_scale
 
         hidden = ctx.enter_context(tc.tile_pool(name="hidden", bufs=2))
         words = ctx.enter_context(tc.tile_pool(name="words", bufs=4))
-        pieces = ctx.enter_context(tc.tile_pool(name="pieces", bufs=2 * PRODUCT_BANKS))
+        pieces = ctx.enter_context(tc.tile_pool(name="pieces", bufs=3 * PRODUCT_BANKS))
         results = ctx.enter_context(tc.tile_pool(name="results", bufs=ROW_TILES * HALVES))
 
         banks = ctx.enter_context(tc.psum_pool(name="banks", bufs=PRODUCT_BANKS))
@@ -277,6 +277,7 @@ def tile_nonlocalmp_pa_kernel(tc, F, W1_words, W1_scales, b1, W2_words, W2_scale
         nc.scalar.copy(out=bias_whole[:], in_=b2_turned[:, 0:C_TILES])
 
         out_rows = out.flatten_outer_dims()
+        bank_pieces = {}
         leaky_pieces = {}
 
         all_banks = list(range(PRODUCT_BANKS))
@@ -285,6 +286,7 @@ def tile_nonlocalmp_pa_kernel(tc, F, W1_words, W1_scales, b1, W2_words, W2_scale
 
         def multiply(step, one_piece):
             codes, planes = h_words[step]
+            bank_pieces[step] = []
             leaky_pieces[step] = []
             for bank in range(PRODUCT_BANKS):
                 product = banks.tile([P, TILES_A_BANK, PAIRS], F32, tag="bank")
@@ -331,24 +333,26 @@ def tile_nonlocalmp_pa_kernel(tc, F, W1_words, W1_scales, b1, W2_words, W2_scale
                             bias=bias_steep[:, c_tile : c_tile + 1],
                             scale=1.0 - SLOPE,
                         )
-                leaky_pieces[step].append((steep,) if one_piece else (steep, flat))
+                bank_pieces[step].append((steep, flat))
+                whole = (steep,) if one_piece else (steep, flat)
+                leaky_pieces[step].append([[piece[:, half, :] for piece in whole] for half in range(HALVES)])
 
         def join_pieces(step):
             for bank in all_banks:
-                steep, flat = leaky_pieces[step][bank]
+                steep, flat = bank_pieces[step][bank]
                 nc.vector.tensor_tensor(out=steep[:], in0=steep[:], in1=flat[:], op=ALU.add)
-                leaky_pieces[step][bank] = (steep,)
+                leaky_pieces[step][bank] = [[steep[:, half, :]] for half in range(HALVES)]
 
         def add_up(step, some_banks):
             r, of_tile = divmod(step, STEPS_A_TILE)
             for bank in some_banks:
-                pieces_here = leaky_pieces[step][bank]
-                for j in range(J_STEP):
-                    for half in range(HALVES):
+                for half in range(HALVES):
+                    pieces_here = leaky_pieces[step][bank][half]
+                    for j in range(J_STEP):
                         for n, piece in enumerate(pieces_here):
                             nc.tensor.matmul(
                                 out=sums[(r, half)][:, bank * P : (bank + 1) * P],
-                                lhsT=piece[:, half, j * P : (j + 1) * P],
+                                lhsT=piece[:, j * P : (j + 1) * P],
                                 rhs=identity[:],
                                 is_transpose=True,
                                 start=(of_tile == 0 and bank == 0 and j == 0 and n == 0),
@@ -368,9 +372,21 @@ def tile_nonlocalmp_pa_kernel(tc, F, W1_words, W1_scales, b1, W2_words, W2_scale
         joined = STEPS - 2
         tile_end = STEPS_A_TILE - 1
 
+        def by_gpsimd(step):
+            return 0 <= step < joined - 1 and step != tile_end
+
+        def join_on_gpsimd(step, half, unit):
+            nc.gpsimd.memset(h_sum[unit][:, 0, 0, 0, 0:1], 0.0)
+            steep, flat = leaky_pieces[step][-1][half]
+            nc.gpsimd.tensor_tensor(out=steep, in0=steep, in1=flat, op=ALU.add)
+            leaky_pieces[step][-1][half] = [steep]
+
         def sum_up(step):
+            if by_gpsimd(step - 2):
+                add_up(step - 2, all_banks[-1:])
             if step > 0:
-                add_up(step - 1, late_banks if step - 1 < joined and step - 1 != tile_end + 1 else all_banks)
+                before = late_banks if step - 1 < joined and step - 1 != tile_end + 1 else all_banks
+                add_up(step - 1, before[:-1] if by_gpsimd(step - 1) else before)
                 if step - 1 == tile_end:
                     for half in range(HALVES):
                         store(0, half, nc.scalar.copy)
@@ -388,6 +404,9 @@ def tile_nonlocalmp_pa_kernel(tc, F, W1_words, W1_scales, b1, W2_words, W2_scale
             quantise(units[n - 1])
             if n < len(units):
                 leaky_and_round(units[n])
+                step, half = divmod(n - 5, HALVES)
+                if by_gpsimd(step):
+                    join_on_gpsimd(step, half, units[n])
             if units[n - 1] == (tile_end, 0):
                 turn_a(1, 1)
                 sum_up(tile_end - 1)
@@ -403,11 +422,11 @@ def tile_nonlocalmp_pa_kernel(tc, F, W1_words, W1_scales, b1, W2_words, W2_scale
         last = STEPS - 1
         for half in range(HALVES):
             for bank in all_banks:
-                (piece,) = leaky_pieces[last][bank]
+                (piece,) = leaky_pieces[last][bank][half]
                 for j in range(J_STEP):
                     nc.tensor.matmul(
                         out=sums[(1, half)][:, bank * P : (bank + 1) * P],
-                        lhsT=piece[:, half, j * P : (j + 1) * P],
+                        lhsT=piece[:, j * P : (j + 1) * P],
                         rhs=identity[:],
                         is_transpose=True,
                         start=False,

@@ -36,6 +36,7 @@ PRODUCT_BANKS = C_TILES // TILES_A_BANK
 SLOPE = 0.2
 WARM_BEFORE_F = 4
 WARM_BEHIND_F = 2
+WARM_BEHIND_HALF = 2
 
 FLOPS = 2 * ROWS * (2 * C) * C + 2 * ROWS * NODES * C * C
 
@@ -77,7 +78,7 @@ def tile_nonlocalmp_pa_kernel(tc, F, W1_words, W1_scales, b1, W2_words, W2_scale
                 nc.sync.dma_start(out=w1_words[:, of_part, cols].bitcast(I32), in_=w1_source[:, of_part, cols])
 
         b1_row = keep.tile([P, C], BF16)
-        nc.vector.memset(b1_row[:], 0.0)
+        nc.vector.memset(b1_row[:].bitcast(I32), 0)
         nc.scalar.dma_start(out=b1_row[0:1, :], in_=b1.rearrange("(o c) -> o c", o=1))
         ones = keep.tile([P, P], BF16)
         nc.gpsimd.memset(ones[:], 1.0)
@@ -96,6 +97,7 @@ def tile_nonlocalmp_pa_kernel(tc, F, W1_words, W1_scales, b1, W2_words, W2_scale
         bias_steep = keep.tile([P, C_TILES], F32)
         bias_flat = keep.tile([P, C_TILES], F32)
         bias_whole = keep.tile([P, C_TILES], F32)
+        bias_sum = keep.tile([P, C_TILES], F32)
 
         hidden = ctx.enter_context(tc.tile_pool(name="hidden", bufs=2))
         words = ctx.enter_context(tc.tile_pool(name="words", bufs=4))
@@ -120,7 +122,7 @@ def tile_nonlocalmp_pa_kernel(tc, F, W1_words, W1_scales, b1, W2_words, W2_scale
             step, g = unit
             r, of_tile = divmod(step, STEPS_A_TILE)
             if first == 0:
-                total = hidden.tile([P, J_STEP, TILE_SETS, NODES, PACK], F32, name="h_sum")
+                total = hidden.tile([P, J_STEP, TILE_SETS, NODES, PACK], F32, name="h_sum", bufs=3)
                 h_sum[unit] = total
             a_view = a_t[(r, g)][:].rearrange("p t (b i) -> p b i t", b=TILE_SETS)
             b_view = b_t[:, r, g, of_tile * J_STEP + first : of_tile * J_STEP + last]
@@ -249,7 +251,15 @@ def tile_nonlocalmp_pa_kernel(tc, F, W1_words, W1_scales, b1, W2_words, W2_scale
         turn_b(0, 0)
         turn_a(0, 0)
         copy_b(0, 0, nc.vector.tensor_copy)
+        b2_turned = banks.tile([P, P], F32, tag="bank")
+        nc.tensor.transpose(b2_turned[:], b2_wide[:], identity[:])
+        nc.scalar.mul(out=bias_sum[:], in_=b2_turned[:, 0:C_TILES], mul=SLOPE * NODES)
+        nc.scalar.mul(out=bias_steep[:], in_=b2_turned[:, 0:C_TILES], mul=1.0 - SLOPE)
+        nc.scalar.mul(out=bias_flat[:], in_=b2_turned[:, 0:C_TILES], mul=SLOPE)
+        nc.scalar.copy(out=bias_whole[:], in_=b2_turned[:, 0:C_TILES])
+        keep_warm(WARM_BEHIND_HALF)
         add_pairs(units[0])
+        add_pairs(units[2], 0, 1)
         leaky_and_round(units[0])
         first_layer(1, 0, 1, on_vector=False)
         first_layer(0, 0, 1, on_vector=False)
@@ -265,24 +275,43 @@ def tile_nonlocalmp_pa_kernel(tc, F, W1_words, W1_scales, b1, W2_words, W2_scale
         for half in range(HALVES):
             turn_b(1, half)
             copy_b(1, half, nc.scalar.copy)
-        add_pairs(units[2], 0, 1)
-        quantise(units[1])
         add_pairs(units[2], 1, J_STEP)
+        quantise(units[1])
         leaky_and_round(units[2])
 
-        b2_turned = banks.tile([P, P], F32, tag="bank")
-        nc.tensor.transpose(b2_turned[:], b2_wide[:], identity[:])
-        nc.scalar.mul(out=bias_steep[:], in_=b2_turned[:, 0:C_TILES], mul=1.0 - SLOPE)
-        nc.scalar.mul(out=bias_flat[:], in_=b2_turned[:, 0:C_TILES], mul=SLOPE)
-        nc.scalar.copy(out=bias_whole[:], in_=b2_turned[:, 0:C_TILES])
+        def spread(target, c_tile, start, stop):
+            nc.tensor.matmul(
+                out=target,
+                lhsT=bias_sum[:, c_tile : c_tile + 1].to_broadcast([P, P]),
+                rhs=identity[:],
+                is_transpose=True,
+                start=start,
+                stop=stop,
+            )
+
+        lacking = keep.tile([P, HALVES, BANK], F32)
+        for half in range(HALVES):
+            spread_row = banks.tile([P, BANK], F32, tag="bank")
+            for quarter in range(QUAD):
+                spread(
+                    spread_row[:, quarter * P : (quarter + 1) * P],
+                    half * QUAD + quarter,
+                    start=(quarter == 0),
+                    stop=(quarter == QUAD - 1),
+                )
+            nc.scalar.mul(out=lacking[:, half], in_=spread_row[:], mul=1.0 - J_STEP / NODES)
 
         out_rows = out.flatten_outer_dims()
         bank_pieces = {}
         leaky_pieces = {}
 
+        last = STEPS - 1
         all_banks = list(range(PRODUCT_BANKS))
         early_banks = all_banks[: PRODUCT_BANKS // 2]
         late_banks = all_banks[PRODUCT_BANKS // 2 :]
+
+        def output_tile(step, bank, k):
+            return TILES_A_BANK * bank + k if step == last else bank + k * PRODUCT_BANKS
 
         def multiply(step, one_piece):
             codes, planes = h_words[step]
@@ -293,7 +322,7 @@ def tile_nonlocalmp_pa_kernel(tc, F, W1_words, W1_scales, b1, W2_words, W2_scale
                 steep = pieces.tile([P, TILES_A_BANK, PAIRS], F32, name="steep")
                 flat = pieces.tile([P, TILES_A_BANK, PAIRS], F32, name="flat")
                 for k in range(TILES_A_BANK):
-                    c_tile = bank + k * PRODUCT_BANKS
+                    c_tile = output_tile(step, bank, k)
                     m_cols = slice(c_tile * P, (c_tile + 1) * P)
                     for g in range(PASSES):
                         nc.tensor.matmul_mx(
@@ -305,17 +334,20 @@ def tile_nonlocalmp_pa_kernel(tc, F, W1_words, W1_scales, b1, W2_words, W2_scale
                             start=(g == 0),
                             stop=(g == PASSES - 1),
                         )
+                if one_piece:
+                    for k in range(TILES_A_BANK):
+                        c_tile = output_tile(step, bank, k)
+                        nc.scalar.activation(
+                            out=flat[:, k, :],
+                            in_=product[:, k, :],
+                            func=ACT.Identity,
+                            bias=bias_flat[:, c_tile : c_tile + 1],
+                            scale=SLOPE,
+                        )
+                else:
+                    nc.scalar.mul(out=flat[:], in_=product[:], mul=SLOPE)
                 for k in range(TILES_A_BANK):
-                    c_tile = bank + k * PRODUCT_BANKS
-                    nc.scalar.activation(
-                        out=flat[:, k, :],
-                        in_=product[:, k, :],
-                        func=ACT.Identity,
-                        bias=bias_flat[:, c_tile : c_tile + 1],
-                        scale=SLOPE,
-                    )
-                for k in range(TILES_A_BANK):
-                    c_tile = bank + k * PRODUCT_BANKS
+                    c_tile = output_tile(step, bank, k)
                     if one_piece:
                         nc.vector.scalar_tensor_tensor(
                             out=steep[:, k, :],
@@ -338,7 +370,7 @@ def tile_nonlocalmp_pa_kernel(tc, F, W1_words, W1_scales, b1, W2_words, W2_scale
                 leaky_pieces[step].append([[piece[:, half, :] for piece in whole] for half in range(HALVES)])
 
         def join_pieces(step):
-            for bank in all_banks:
+            for bank in all_banks[1:]:
                 steep, flat = bank_pieces[step][bank]
                 nc.vector.tensor_tensor(out=steep[:], in0=steep[:], in1=flat[:], op=ALU.add)
                 leaky_pieces[step][bank] = [[steep[:, half, :]] for half in range(HALVES)]
@@ -355,7 +387,7 @@ def tile_nonlocalmp_pa_kernel(tc, F, W1_words, W1_scales, b1, W2_words, W2_scale
                                 lhsT=piece[:, j * P : (j + 1) * P],
                                 rhs=identity[:],
                                 is_transpose=True,
-                                start=(of_tile == 0 and bank == 0 and j == 0 and n == 0),
+                                start=(r == 1 and of_tile == 0 and bank == 0 and j == 0 and n == 0),
                                 stop=(
                                     of_tile == STEPS_A_TILE - 1
                                     and bank == PRODUCT_BANKS - 1
@@ -364,16 +396,18 @@ def tile_nonlocalmp_pa_kernel(tc, F, W1_words, W1_scales, b1, W2_words, W2_scale
                                 ),
                             )
 
-        def store(r, half, copy):
+        def store(r, half):
             result = results.tile([P, BANK], F32, name="result")
-            copy(out=result[:], in_=sums[(r, half)][:])
+            if r == 0:
+                nc.scalar.copy(out=result[:], in_=sums[(r, half)][:])
+            else:
+                nc.vector.tensor_tensor(out=result[:], in0=sums[(r, half)][:], in1=lacking[:, half], op=ALU.add)
             nc.sync.dma_start(out=out_rows[r * P : (r + 1) * P, half * BANK : (half + 1) * BANK], in_=result[:])
 
-        joined = STEPS - 2
         tile_end = STEPS_A_TILE - 1
 
         def by_gpsimd(step):
-            return 0 <= step < joined - 1 and step != tile_end
+            return 0 <= step < last - 2 and step != tile_end
 
         def join_on_gpsimd(step, half, unit):
             nc.gpsimd.memset(h_sum[unit][:, 0, 0, 0, 0:1], 0.0)
@@ -385,17 +419,24 @@ def tile_nonlocalmp_pa_kernel(tc, F, W1_words, W1_scales, b1, W2_words, W2_scale
             if by_gpsimd(step - 2):
                 add_up(step - 2, all_banks[-1:])
             if step > 0:
-                before = late_banks if step - 1 < joined and step - 1 != tile_end + 1 else all_banks
+                before = all_banks if step - 1 == tile_end + 1 else all_banks[1:] if step == last else late_banks
                 add_up(step - 1, before[:-1] if by_gpsimd(step - 1) else before)
                 if step - 1 == tile_end:
                     for half in range(HALVES):
-                        store(0, half, nc.scalar.copy)
+                        store(0, half)
                         open_sum(1, half)
-            if step < joined and step != tile_end + 1:
-                add_up(step, early_banks)
+            if step < last and step != tile_end + 1:
+                add_up(step, all_banks[:1] if step == last - 1 else early_banks)
 
         for half in range(HALVES):
             open_sum(0, half)
+            for quarter in range(QUAD):
+                spread(
+                    sums[(0, half)][:, quarter * P : (quarter + 1) * P],
+                    half * QUAD + quarter,
+                    start=(quarter == 0),
+                    stop=False,
+                )
         multiply(0, one_piece=False)
         sum_up(0)
         for n in range(3, len(units) + 1):
@@ -412,25 +453,25 @@ def tile_nonlocalmp_pa_kernel(tc, F, W1_words, W1_scales, b1, W2_words, W2_scale
                 sum_up(tile_end - 1)
             if n % PASSES == 0:
                 step = n // PASSES - 1
-                if step == STEPS - 1:
+                if step == last:
                     join_pieces(step - 1)
                 if step == tile_end - 1:
                     turn_a(1, 0)
-                multiply(step, one_piece=(step == STEPS - 1))
+                multiply(step, one_piece=(step == last))
                 if step != tile_end - 1:
                     sum_up(step)
-        last = STEPS - 1
-        for half in range(HALVES):
-            for bank in all_banks:
-                (piece,) = leaky_pieces[last][bank][half]
+        for bank in all_banks:
+            for k in range(TILES_A_BANK):
+                half, quarter = divmod(output_tile(last, bank, k), QUAD)
+                (piece,) = leaky_pieces[last][bank][k]
                 for j in range(J_STEP):
                     nc.tensor.matmul(
-                        out=sums[(1, half)][:, bank * P : (bank + 1) * P],
+                        out=sums[(1, half)][:, quarter * P : (quarter + 1) * P],
                         lhsT=piece[:, j * P : (j + 1) * P],
                         rhs=identity[:],
                         is_transpose=True,
                         start=False,
-                        stop=(bank == PRODUCT_BANKS - 1 and j == J_STEP - 1),
+                        stop=(quarter == QUAD - 1 and j == J_STEP - 1),
                     )
         for half in range(HALVES):
-            store(1, half, nc.vector.tensor_copy if half == 0 else nc.scalar.copy)
+            store(1, half)

@@ -34,7 +34,8 @@ STEPS = ROW_TILES * STEPS_A_TILE
 TILES_A_BANK = BANK // PAIRS
 PRODUCT_BANKS = C_TILES // TILES_A_BANK
 SLOPE = 0.2
-WARM_BEFORE_F = 4
+VECTOR_SETS = 5
+WARM_BEFORE_F = 3
 WARM_BEHIND_F = 2
 WARM_BEHIND_HALF = 2
 
@@ -57,7 +58,9 @@ def tile_nonlocalmp_pa_kernel(tc, F, W1_words, W1_scales, b1, W2_words, W2_scale
         nc.vector.memset(w2_planes[:].bitcast(I32), 0)
 
         f_rows = keep.tile([P, ROW_TILES, C], BF16)
-        nc.scalar.dma_start(out=f_rows[:], in_=F.flatten_outer_dims().rearrange("(r p) c -> p r c", p=P))
+        f_source = F.flatten_outer_dims().rearrange("(r p) c -> p r c", p=P)
+        for r in range(ROW_TILES):
+            nc.scalar.dma_start(out=f_rows[:, r], in_=f_source[:, r])
 
         def load_planes(planes, scales, passes):
             scale_rows = scales.bitcast(I32)
@@ -69,6 +72,13 @@ def tile_nonlocalmp_pa_kernel(tc, F, W1_words, W1_scales, b1, W2_words, W2_scale
                 )
 
         load_planes(w1_planes, W1_scales, 2 * PASSES)
+        b1_row = keep.tile([P, C], BF16)
+        nc.vector.memset(b1_row[:].bitcast(I32), 0)
+        ones = keep.tile([P, P], BF16)
+        nc.scalar.add(ones[:], zeros[:, 0:P], 1.0)
+        b2_rows = keep.tile([P, P], BF16)
+        nc.vector.memset(b2_rows[:], 0.0)
+
         w1_words = keep.tile([P, 2 * PASSES, C], U32, align_bytes=64)
         w1_source = W1_words.rearrange("g p n t -> p g (n t)").bitcast(I32)
         for half in range(HALVES):
@@ -76,19 +86,16 @@ def tile_nonlocalmp_pa_kernel(tc, F, W1_words, W1_scales, b1, W2_words, W2_scale
             for part in (1, 0):
                 of_part = slice(PASSES * part, PASSES * (part + 1))
                 nc.sync.dma_start(out=w1_words[:, of_part, cols].bitcast(I32), in_=w1_source[:, of_part, cols])
-
-        b1_row = keep.tile([P, C], BF16)
-        nc.vector.memset(b1_row[:].bitcast(I32), 0)
-        nc.scalar.dma_start(out=b1_row[0:1, :], in_=b1.rearrange("(o c) -> o c", o=1))
-        ones = keep.tile([P, P], BF16)
-        nc.gpsimd.memset(ones[:], 1.0)
-        b2_rows = keep.tile([P, P], BF16)
-        nc.vector.memset(b2_rows[:], 0.0)
-        nc.scalar.dma_start(out=b2_rows[0:C_TILES, :], in_=b2.rearrange("(c p) -> c p", p=P))
+            if half == 0:
+                nc.sync.dma_start(out=b1_row[0:1, :], in_=b1.rearrange("(o c) -> o c", o=1))
+                nc.sync.dma_start(out=b2_rows[0:C_TILES, :], in_=b2.rearrange("(c p) -> c p", p=P))
 
         load_planes(w2_planes, W2_scales, PASSES)
         w2_words = keep.tile([P, PASSES, C], U32, align_bytes=64)
         nc.sync.dma_start(out=w2_words[:].bitcast(I32), in_=W2_words.rearrange("g p n t -> p g (n t)").bitcast(I32))
+
+        b2_everywhere = keep.tile([P, C], BF16)
+        nc.sync.dma_start(out=b2_everywhere[:], in_=b2.partition_broadcast(P))
 
         identity = keep.tile([P, P], F32)
         make_identity(nc, identity[:])
@@ -109,6 +116,7 @@ def tile_nonlocalmp_pa_kernel(tc, F, W1_words, W1_scales, b1, W2_words, W2_scale
         sum_banks = ctx.enter_context(tc.psum_pool(name="sum_banks", bufs=1))
 
         a_t = {}
+        a_side = keep.tile([P, ROW_TILES, TILE_SETS - VECTOR_SETS, NODES, PACK], F32)
         sums = {}
 
         def open_sum(r, half):
@@ -118,25 +126,37 @@ def tile_nonlocalmp_pa_kernel(tc, F, W1_words, W1_scales, b1, W2_words, W2_scale
         h_rounded = {}
         h_words = {}
 
-        def add_pairs(unit, first=0, last=J_STEP):
+        def open_unit(unit, slots_of=None):
+            g = unit[1] if slots_of is None else slots_of
+            total = hidden.tile([P, J_STEP, TILE_SETS, NODES, PACK], F32, name="h_sum_%d" % g, bufs=2 - g)
+            h_sum[unit] = total
+
+        def add_pairs(unit, first=0, last=J_STEP, sets=TILE_SETS):
             step, g = unit
             r, of_tile = divmod(step, STEPS_A_TILE)
-            if first == 0:
-                total = hidden.tile([P, J_STEP, TILE_SETS, NODES, PACK], F32, name="h_sum", bufs=3)
-                h_sum[unit] = total
-            a_view = a_t[(r, g)][:].rearrange("p t (b i) -> p b i t", b=TILE_SETS)
-            b_view = b_t[:, r, g, of_tile * J_STEP + first : of_tile * J_STEP + last]
-            shape = [P, last - first, TILE_SETS, NODES, PACK]
+            a_view = a_t[(r, g)][:].rearrange("p t (b i) -> p b i t", b=TILE_SETS)[:, 0:sets]
+            b_view = b_t[:, r, g, of_tile * J_STEP + first : of_tile * J_STEP + last, 0:sets]
+            shape = [P, last - first, sets, NODES, PACK]
             nc.vector.tensor_tensor(
-                out=h_sum[unit][:, first:last],
+                out=h_sum[unit][:, first:last, 0:sets],
                 in0=a_view.unsqueeze(1).to_broadcast(shape),
                 in1=b_view.unsqueeze(3).to_broadcast(shape),
                 op=ALU.add,
             )
 
+        def add_on_gpsimd(step):
+            r, of_tile = divmod(step, STEPS_A_TILE)
+            b_view = b_t[:, r, 1, (of_tile + 1) * J_STEP - 1, VECTOR_SETS:]
+            nc.gpsimd.tensor_tensor(
+                out=h_sum[(step, 1)][:, J_STEP - 1, VECTOR_SETS:],
+                in0=a_side[:, r],
+                in1=b_view.unsqueeze(2).to_broadcast([P, TILE_SETS - VECTOR_SETS, NODES, PACK]),
+                op=ALU.add,
+            )
+
         def leaky_and_round(unit):
             total = h_sum[unit][:].rearrange("p j b n t -> p (j b n t)")
-            rounded = hidden.tile([P, PAIRS * PACK], BF16, name="h_rounded", align_bytes=64)
+            rounded = hidden.tile([P, PAIRS * PACK], BF16, name="h_rounded", align_bytes=64, bufs=3)
             nc.vector.scalar_tensor_tensor(
                 out=rounded[:], in0=total, scalar=SLOPE, in1=total, op0=ALU.mult, op1=ALU.max
             )
@@ -161,8 +181,8 @@ def tile_nonlocalmp_pa_kernel(tc, F, W1_words, W1_scales, b1, W2_words, W2_scale
         keep_warm(WARM_BEFORE_F)
         f_codes = keep.tile([P, ROW_TILES, PASSES, P], U32, align_bytes=64)
         f_planes = keep.tile([P, ROW_TILES, PASSES, P], U8, align_bytes=64)
-        f_grouped = []
-        for r in range(ROW_TILES):
+
+        def group_f(r, copy_words):
             turned = banks.tile([P, PASSES, 2, P], F32, tag="bank")
             for g in range(PASSES):
                 for u in range(2):
@@ -170,22 +190,21 @@ def tile_nonlocalmp_pa_kernel(tc, F, W1_words, W1_scales, b1, W2_words, W2_scale
                         turned[:, g, u, :], f_words[:, r, 256 * g + u : 256 * (g + 1) : 2], identity[:]
                     )
             grouped = stage.tile([P, ROWS * PACK], BF16, name="f_grouped", align_bytes=64)
-            copy_words = nc.vector.tensor_copy if r == 0 else nc.scalar.copy
             copy_words(
                 out=grouped[:].bitcast(F32).rearrange("p (g n u) -> p g n u", g=PASSES, u=2),
                 in_=turned[:].rearrange("p g u n -> p g n u"),
             )
-            f_grouped.append(grouped)
-        keep_warm(WARM_BEHIND_F)
-        for r in range(ROW_TILES):
+            return grouped
+
+        def quantise_f(r, grouped):
             nc.vector.quantize_mx(
                 out=f_codes[:, r].rearrange("p g n -> p (g n)").bitcast(FP8X4),
                 scales=f_planes[:, r].rearrange("p g n -> p (g n)"),
-                in_=f_grouped[r][:],
+                in_=grouped[:],
             )
-        b2_wide = keep.tile([P, P], F32)
-        nc.scalar.copy(out=b2_wide[:], in_=b2_rows[:])
 
+        quantise_f(0, group_f(0, nc.vector.tensor_copy))
+        keep_warm(WARM_BEHIND_F)
         sorted_rows = {}
 
         def first_layer(part, r, half, on_vector):
@@ -211,6 +230,11 @@ def tile_nonlocalmp_pa_kernel(tc, F, W1_words, W1_scales, b1, W2_words, W2_scale
             a_t[(r, half)] = a_banks.tile([P, PACK, P], F32, name="a_%d" % half)
             for t in range(PACK):
                 nc.tensor.transpose(a_t[(r, half)][:, t, :], sorted_rows[(0, r, half)][:, t, :], identity[:])
+            if half == 1:
+                nc.scalar.copy(
+                    out=a_side[:, r].rearrange("p b i t -> p (b i) t"),
+                    in_=a_t[(r, half)][:, :, VECTOR_SETS * NODES :].rearrange("p t n -> p n t"),
+                )
 
         b_turned = {}
 
@@ -250,22 +274,29 @@ def tile_nonlocalmp_pa_kernel(tc, F, W1_words, W1_scales, b1, W2_words, W2_scale
         first_layer(0, 0, 0, on_vector=False)
         turn_b(0, 0)
         turn_a(0, 0)
+        f_grouped_1 = group_f(1, nc.scalar.copy)
+        b2_wide = keep.tile([P, P], F32)
+        nc.scalar.copy(out=b2_wide[:], in_=b2_rows[:])
         copy_b(0, 0, nc.vector.tensor_copy)
+        keep_warm(WARM_BEHIND_HALF)
+        open_unit(units[0])
+        add_pairs(units[0])
+        open_unit(units[2])
+        add_pairs(units[2])
+        leaky_and_round(units[0])
+        quantise_f(1, f_grouped_1)
+        first_layer(1, 0, 1, on_vector=False)
+        first_layer(0, 0, 1, on_vector=False)
+        turn_b(0, 1)
+        turn_a(0, 1)
+        copy_b(0, 1, nc.scalar.copy)
         b2_turned = banks.tile([P, P], F32, tag="bank")
         nc.tensor.transpose(b2_turned[:], b2_wide[:], identity[:])
         nc.scalar.mul(out=bias_sum[:], in_=b2_turned[:, 0:C_TILES], mul=SLOPE * NODES)
         nc.scalar.mul(out=bias_steep[:], in_=b2_turned[:, 0:C_TILES], mul=1.0 - SLOPE)
         nc.scalar.mul(out=bias_flat[:], in_=b2_turned[:, 0:C_TILES], mul=SLOPE)
         nc.scalar.copy(out=bias_whole[:], in_=b2_turned[:, 0:C_TILES])
-        keep_warm(WARM_BEHIND_HALF)
-        add_pairs(units[0])
-        add_pairs(units[2], 0, 1)
-        leaky_and_round(units[0])
-        first_layer(1, 0, 1, on_vector=False)
-        first_layer(0, 0, 1, on_vector=False)
-        turn_b(0, 1)
-        turn_a(0, 1)
-        copy_b(0, 1, nc.scalar.copy)
+        open_unit(units[1])
         add_pairs(units[1])
         quantise(units[0])
         leaky_and_round(units[1])
@@ -275,9 +306,13 @@ def tile_nonlocalmp_pa_kernel(tc, F, W1_words, W1_scales, b1, W2_words, W2_scale
         for half in range(HALVES):
             turn_b(1, half)
             copy_b(1, half, nc.scalar.copy)
-        add_pairs(units[2], 1, J_STEP)
+        open_unit(units[3], slots_of=0)
+        add_pairs(units[3], 0, 1)
         quantise(units[1])
         leaky_and_round(units[2])
+        add_pairs(units[3], 1, J_STEP)
+        quantise(units[2])
+        leaky_and_round(units[3])
 
         def spread(target, c_tile, start, stop):
             nc.tensor.matmul(
@@ -288,18 +323,6 @@ def tile_nonlocalmp_pa_kernel(tc, F, W1_words, W1_scales, b1, W2_words, W2_scale
                 start=start,
                 stop=stop,
             )
-
-        lacking = keep.tile([P, HALVES, BANK], F32)
-        for half in range(HALVES):
-            spread_row = banks.tile([P, BANK], F32, tag="bank")
-            for quarter in range(QUAD):
-                spread(
-                    spread_row[:, quarter * P : (quarter + 1) * P],
-                    half * QUAD + quarter,
-                    start=(quarter == 0),
-                    stop=(quarter == QUAD - 1),
-                )
-            nc.scalar.mul(out=lacking[:, half], in_=spread_row[:], mul=1.0 - J_STEP / NODES)
 
         out_rows = out.flatten_outer_dims()
         bank_pieces = {}
@@ -369,12 +392,6 @@ def tile_nonlocalmp_pa_kernel(tc, F, W1_words, W1_scales, b1, W2_words, W2_scale
                 whole = (steep,) if one_piece else (steep, flat)
                 leaky_pieces[step].append([[piece[:, half, :] for piece in whole] for half in range(HALVES)])
 
-        def join_pieces(step):
-            for bank in all_banks[1:]:
-                steep, flat = bank_pieces[step][bank]
-                nc.vector.tensor_tensor(out=steep[:], in0=steep[:], in1=flat[:], op=ALU.add)
-                leaky_pieces[step][bank] = [[steep[:, half, :]] for half in range(HALVES)]
-
         def add_up(step, some_banks):
             r, of_tile = divmod(step, STEPS_A_TILE)
             for bank in some_banks:
@@ -401,19 +418,25 @@ def tile_nonlocalmp_pa_kernel(tc, F, W1_words, W1_scales, b1, W2_words, W2_scale
             if r == 0:
                 nc.scalar.copy(out=result[:], in_=sums[(r, half)][:])
             else:
-                nc.vector.tensor_tensor(out=result[:], in0=sums[(r, half)][:], in1=lacking[:, half], op=ALU.add)
+                nc.vector.scalar_tensor_tensor(
+                    out=result[:],
+                    in0=b2_everywhere[:, half * BANK : (half + 1) * BANK],
+                    scalar=SLOPE * (NODES - J_STEP),
+                    in1=sums[(r, half)][:],
+                    op0=ALU.mult,
+                    op1=ALU.add,
+                )
             nc.sync.dma_start(out=out_rows[r * P : (r + 1) * P, half * BANK : (half + 1) * BANK], in_=result[:])
 
         tile_end = STEPS_A_TILE - 1
 
         def by_gpsimd(step):
-            return 0 <= step < last - 2 and step != tile_end
+            return 0 <= step < last - 3 and step != tile_end
 
-        def join_on_gpsimd(step, half, unit):
-            nc.gpsimd.memset(h_sum[unit][:, 0, 0, 0, 0:1], 0.0)
-            steep, flat = leaky_pieces[step][-1][half]
-            nc.gpsimd.tensor_tensor(out=steep, in0=steep, in1=flat, op=ALU.add)
-            leaky_pieces[step][-1][half] = [steep]
+        def join(step, bank, add):
+            steep, flat = bank_pieces[step][bank]
+            add(out=steep[:], in0=steep[:], in1=flat[:], op=ALU.add)
+            leaky_pieces[step][bank] = [[steep[:, half, :]] for half in range(HALVES)]
 
         def sum_up(step):
             if by_gpsimd(step - 2):
@@ -439,27 +462,37 @@ def tile_nonlocalmp_pa_kernel(tc, F, W1_words, W1_scales, b1, W2_words, W2_scale
                 )
         multiply(0, one_piece=False)
         sum_up(0)
-        for n in range(3, len(units) + 1):
-            if n < len(units):
-                add_pairs(units[n])
-            quantise(units[n - 1])
-            if n < len(units):
-                leaky_and_round(units[n])
-                step, half = divmod(n - 5, HALVES)
-                if by_gpsimd(step):
-                    join_on_gpsimd(step, half, units[n])
-            if units[n - 1] == (tile_end, 0):
-                turn_a(1, 1)
-                sum_up(tile_end - 1)
-            if n % PASSES == 0:
-                step = n // PASSES - 1
-                if step == last:
-                    join_pieces(step - 1)
-                if step == tile_end - 1:
-                    turn_a(1, 0)
-                multiply(step, one_piece=(step == last))
-                if step != tile_end - 1:
-                    sum_up(step)
+        for step in range(2, STEPS):
+            first, second = (step, 0), (step, 1)
+            open_unit(first)
+            open_unit(second)
+            add_pairs(first)
+            together = 2 < step < last
+            if together:
+                add_pairs(second, 0, J_STEP - 1)
+                add_pairs(second, J_STEP - 1, J_STEP, VECTOR_SETS)
+                add_on_gpsimd(step)
+                if by_gpsimd(step - 3):
+                    join(step - 3, all_banks[-1], nc.gpsimd.tensor_tensor)
+            if step == tile_end:
+                for half in range(HALVES):
+                    turn_a(1, half)
+            quantise((step - 1, 1))
+            multiply(step - 1, one_piece=False)
+            sum_up(step - 1)
+            leaky_and_round(first)
+            if together:
+                leaky_and_round(second)
+                quantise(first)
+            else:
+                add_pairs(second)
+                quantise(first)
+                leaky_and_round(second)
+        quantise((last, 1))
+        for bank in all_banks[1:]:
+            join(last - 1, bank, nc.vector.tensor_tensor)
+        multiply(last, one_piece=True)
+        sum_up(last)
         for bank in all_banks:
             for k in range(TILES_A_BANK):
                 half, quarter = divmod(output_tile(last, bank, k), QUAD)

from contextlib import ExitStack

import concourse.mybir as mybir
from concourse.masks import make_identity

F32 = mybir.dt.float32
BF16 = mybir.dt.bfloat16
I32 = mybir.dt.int32
U32 = mybir.dt.uint32
U8 = mybir.dt.uint8
FP8X4 = mybir.dt.float8_e4m3fn_x4
ACT = mybir.ActivationFunctionType
ALU = mybir.AluOpType

P = 128
PACK = 4
K_PASS = P * PACK
BANK = 512

SETS = 16
NODES = 16
C = 1024
ROWS = SETS * NODES
ROW_TILES = ROWS // P
TILE_SETS = P // NODES
PASSES = C // K_PASS
HALVES = C // BANK
C_TILES = C // P
QUAD = BANK // P
J_STEP = 2
PAIRS = J_STEP * P
STEPS_A_TILE = NODES // J_STEP
STEPS = ROW_TILES * STEPS_A_TILE
TILES_A_BANK = BANK // PAIRS
PRODUCT_BANKS = C_TILES // TILES_A_BANK
SLOPE = 0.2
VECTOR_SETS = 5
WARM_BEFORE_F = 3
WARM_BEHIND_F = 2
WARM_BEHIND_HALF = 2

FLOPS = 2 * ROWS * (2 * C) * C + 2 * ROWS * NODES * C * C


def tile_nonlocalmp_pa_kernel(tc, F, W1_words, W1_scales, b1, W2_words, W2_scales, b2, out):
    nc = tc.nc
    with ExitStack() as ctx:
        ctx.enter_context(tc.manual_schedule())
        keep = ctx.enter_context(tc.tile_pool(name="keep", bufs=1))
        stage = ctx.enter_context(tc.tile_pool(name="stage", bufs=2))

        zeros = keep.tile([P, BANK], BF16)
        nc.gpsimd.memset(zeros[:], 0.0)

        w1_planes = keep.tile([P, C], U8, align_bytes=64)
        w2_planes = keep.tile([P, C], U8, align_bytes=64)
        nc.vector.memset(w1_planes[:].bitcast(I32), 0)
        nc.vector.memset(w2_planes[:].bitcast(I32), 0)

        f_rows = keep.tile([P, ROW_TILES, C], BF16)
        f_source = F.flatten_outer_dims().rearrange("(r p) c -> p r c", p=P)
        for r in range(ROW_TILES):
            nc.scalar.dma_start(out=f_rows[:, r], in_=f_source[:, r])

        def load_planes(planes, scales, passes):
            scale_rows = scales.bitcast(I32)
            for quadrant in range(4):
                first = 32 * quadrant
                nc.sync.dma_start(
                    out=planes[first : first + 4 * passes, :].bitcast(I32),
                    in_=scale_rows[:, 4 * quadrant : 4 * quadrant + 4, :],
                )

        load_planes(w1_planes, W1_scales, 2 * PASSES)
        b1_row = keep.tile([P, C], BF16)
        nc.vector.memset(b1_row[:].bitcast(I32), 0)
        ones = keep.tile([P, P], BF16)
        nc.scalar.add(ones[:], zeros[:, 0:P], 1.0)
        b2_rows = keep.tile([P, P], BF16)
        nc.vector.memset(b2_rows[:], 0.0)

        w1_words = keep.tile([P, 2 * PASSES, C], U32, align_bytes=64)
        w1_source = W1_words.rearrange("g p n t -> p g (n t)").bitcast(I32)
        for half in range(HALVES):
            cols = slice(half * BANK, (half + 1) * BANK)
            for part in (1, 0):
                of_part = slice(PASSES * part, PASSES * (part + 1))
                nc.sync.dma_start(out=w1_words[:, of_part, cols].bitcast(I32), in_=w1_source[:, of_part, cols])
            if half == 0:
                nc.sync.dma_start(out=b1_row[0:1, :], in_=b1.rearrange("(o c) -> o c", o=1))
                nc.sync.dma_start(out=b2_rows[0:C_TILES, :], in_=b2.rearrange("(c p) -> c p", p=P))

        load_planes(w2_planes, W2_scales, PASSES)
        w2_words = keep.tile([P, PASSES, C], U32, align_bytes=64)
        nc.sync.dma_start(out=w2_words[:].bitcast(I32), in_=W2_words.rearrange("g p n t -> p g (n t)").bitcast(I32))

        b2_everywhere = keep.tile([P, C], BF16)
        nc.sync.dma_start(out=b2_everywhere[:], in_=b2.partition_broadcast(P))

        identity = keep.tile([P, P], F32)
        make_identity(nc, identity[:])

        b_t = keep.tile([P, ROW_TILES, PASSES, NODES, TILE_SETS, PACK], F32)
        bias_steep = keep.tile([P, C_TILES], F32)
        bias_flat = keep.tile([P, C_TILES], F32)
        bias_whole = keep.tile([P, C_TILES], F32)
        bias_sum = keep.tile([P, C_TILES], F32)

        hidden = ctx.enter_context(tc.tile_pool(name="hidden", bufs=2))
        words = ctx.enter_context(tc.tile_pool(name="words", bufs=4))
        pieces = ctx.enter_context(tc.tile_pool(name="pieces", bufs=3 * PRODUCT_BANKS))
        results = ctx.enter_context(tc.tile_pool(name="results", bufs=ROW_TILES * HALVES))

        banks = ctx.enter_context(tc.psum_pool(name="banks", bufs=PRODUCT_BANKS))
        a_banks = ctx.enter_context(tc.psum_pool(name="a_banks", bufs=1))
        sum_banks = ctx.enter_context(tc.psum_pool(name="sum_banks", bufs=1))

        a_t = {}
        a_side = keep.tile([P, ROW_TILES, TILE_SETS - VECTOR_SETS, NODES, PACK], F32)
        sums = {}

        def open_sum(r, half):
            sums[(r, half)] = sum_banks.tile([P, BANK], F32, name="sum_%d" % half)

        h_sum = {}
        h_rounded = {}
        h_words = {}

        def open_unit(unit, slots_of=None):
            g = unit[1] if slots_of is None else slots_of
            total = hidden.tile([P, J_STEP, TILE_SETS, NODES, PACK], F32, name="h_sum_%d" % g, bufs=2 - g)
            h_sum[unit] = total

        def add_pairs(unit, first=0, last=J_STEP, sets=TILE_SETS):
            step, g = unit
            r, of_tile = divmod(step, STEPS_A_TILE)
            a_view = a_t[(r, g)][:].rearrange("p t (b i) -> p b i t", b=TILE_SETS)[:, 0:sets]
            b_view = b_t[:, r, g, of_tile * J_STEP + first : of_tile * J_STEP + last, 0:sets]
            shape = [P, last - first, sets, NODES, PACK]
            nc.vector.tensor_tensor(
                out=h_sum[unit][:, first:last, 0:sets],
                in0=a_view.unsqueeze(1).to_broadcast(shape),
                in1=b_view.unsqueeze(3).to_broadcast(shape),
                op=ALU.add,
            )

        def add_on_gpsimd(step):
            r, of_tile = divmod(step, STEPS_A_TILE)
            b_view = b_t[:, r, 1, (of_tile + 1) * J_STEP - 1, VECTOR_SETS:]
            nc.gpsimd.tensor_tensor(
                out=h_sum[(step, 1)][:, J_STEP - 1, VECTOR_SETS:],
                in0=a_side[:, r],
                in1=b_view.unsqueeze(2).to_broadcast([P, TILE_SETS - VECTOR_SETS, NODES, PACK]),
                op=ALU.add,
            )

        def leaky_and_round(unit):
            total = h_sum[unit][:].rearrange("p j b n t -> p (j b n t)")
            rounded = hidden.tile([P, PAIRS * PACK], BF16, name="h_rounded", align_bytes=64, bufs=3)
            nc.vector.scalar_tensor_tensor(
                out=rounded[:], in0=total, scalar=SLOPE, in1=total, op0=ALU.mult, op1=ALU.max
            )
            h_rounded[unit] = rounded

        def quantise(unit):
            step, g = unit
            if step not in h_words:
                codes = words.tile([P, PASSES, PAIRS], U32, name="h_codes", align_bytes=64)
                planes = words.tile([P, PASSES, PAIRS], U8, name="h_planes", align_bytes=64)
                h_words[step] = (codes, planes)
            codes, planes = h_words[step]
            nc.vector.quantize_mx(out=codes[:, g, :].bitcast(FP8X4), scales=planes[:, g, :], in_=h_rounded[unit][:])

        f_words = f_rows[:].bitcast(F32)
        unread = sum_banks.tile([P, BANK], F32, name="sum_0")

        def keep_warm(matmuls):
            for n in range(matmuls):
                nc.tensor.matmul(out=unread[:], lhsT=zeros[:, 0:P], rhs=zeros[:], start=True, stop=True)

        keep_warm(WARM_BEFORE_F)
        f_codes = keep.tile([P, ROW_TILES, PASSES, P], U32, align_bytes=64)
        f_planes = keep.tile([P, ROW_TILES, PASSES, P], U8, align_bytes=64)

        def group_f(r, copy_words):
            turned = banks.tile([P, PASSES, 2, P], F32, tag="bank")
            for g in range(PASSES):
                for u in range(2):
                    nc.tensor.transpose(
                        turned[:, g, u, :], f_words[:, r, 256 * g + u : 256 * (g + 1) : 2], identity[:]
                    )
            grouped = stage.tile([P, ROWS * PACK], BF16, name="f_grouped", align_bytes=64)
            copy_words(
                out=grouped[:].bitcast(F32).rearrange("p (g n u) -> p g n u", g=PASSES, u=2),
                in_=turned[:].rearrange("p g u n -> p g n u"),
            )
            return grouped

        def quantise_f(r, grouped):
            nc.vector.quantize_mx(
                out=f_codes[:, r].rearrange("p g n -> p (g n)").bitcast(FP8X4),
                scales=f_planes[:, r].rearrange("p g n -> p (g n)"),
                in_=grouped[:],
            )

        quantise_f(0, group_f(0, nc.vector.tensor_copy))
        keep_warm(WARM_BEHIND_F)
        sorted_rows = {}

        def first_layer(part, r, half, on_vector):
            cols = slice(half * BANK, (half + 1) * BANK)
            product = banks.tile([P, BANK], F32, tag="bank")
            for g in range(PASSES):
                w1_pass = PASSES * part + g
                nc.tensor.matmul_mx(
                    out=product[:],
                    lhsT=f_codes[:, r, g, :].bitcast(FP8X4),
                    lhsT_scale=f_planes[:, r, g, :],
                    rhs=w1_words[:, w1_pass, cols].bitcast(FP8X4),
                    rhs_scale=w1_planes[4 * w1_pass : P, cols],
                    start=(g == 0),
                    stop=(g == PASSES - 1),
                )
            by_t = keep.tile([P, PACK, P], F32, name="by_t_%d%d%d" % (part, r, half))
            copy_rows = nc.vector.tensor_copy if on_vector else nc.scalar.copy
            copy_rows(out=by_t[:], in_=product[:].rearrange("r (p t) -> r t p", t=PACK))
            sorted_rows[(part, r, half)] = by_t

        def turn_a(r, half):
            a_t[(r, half)] = a_banks.tile([P, PACK, P], F32, name="a_%d" % half)
            for t in range(PACK):
                nc.tensor.transpose(a_t[(r, half)][:, t, :], sorted_rows[(0, r, half)][:, t, :], identity[:])
            if half == 1:
                nc.scalar.copy(
                    out=a_side[:, r].rearrange("p b i t -> p (b i) t"),
                    in_=a_t[(r, half)][:, :, VECTOR_SETS * NODES :].rearrange("p t n -> p n t"),
                )

        b_turned = {}

        def turn_b(r, half):
            if r == 0:
                turned = banks.tile([P, PACK, P], F32, tag="bank")
            else:
                turned = sum_banks.tile([P, PACK, P], F32, name="sum_%d" % half)
            for t in range(PACK):
                nc.tensor.matmul(
                    out=turned[:, t, :],
                    lhsT=b1_row[:, half * BANK + t : (half + 1) * BANK : PACK],
                    rhs=ones[:],
                    start=(t == 0),
                    stop=False,
                )
            for t in range(PACK):
                nc.tensor.matmul(
                    out=turned[:, t, :],
                    lhsT=sorted_rows[(1, r, half)][:, t, :],
                    rhs=identity[:],
                    is_transpose=True,
                    start=False,
                    stop=(t == PACK - 1),
                )
            b_turned[(r, half)] = turned

        def copy_b(r, half, copy):
            copy(
                out=b_t[:, r, half].rearrange("p j b t -> p b j t"),
                in_=b_turned[(r, half)][:].rearrange("p t (b j) -> p b j t", b=TILE_SETS),
            )

        units = [(step, g) for step in range(STEPS) for g in range(PASSES)]

        first_layer(1, 0, 0, on_vector=True)
        first_layer(0, 0, 0, on_vector=False)
        turn_b(0, 0)
        turn_a(0, 0)
        f_grouped_1 = group_f(1, nc.scalar.copy)
        b2_wide = keep.tile([P, P], F32)
        nc.scalar.copy(out=b2_wide[:], in_=b2_rows[:])
        copy_b(0, 0, nc.vector.tensor_copy)
        keep_warm(WARM_BEHIND_HALF)
        open_unit(units[0])
        add_pairs(units[0])
        open_unit(units[2])
        add_pairs(units[2])
        leaky_and_round(units[0])
        quantise_f(1, f_grouped_1)
        first_layer(1, 0, 1, on_vector=False)
        first_layer(0, 0, 1, on_vector=False)
        turn_b(0, 1)
        turn_a(0, 1)
        copy_b(0, 1, nc.scalar.copy)
        b2_turned = banks.tile([P, P], F32, tag="bank")
        nc.tensor.transpose(b2_turned[:], b2_wide[:], identity[:])
        nc.scalar.mul(out=bias_sum[:], in_=b2_turned[:, 0:C_TILES], mul=SLOPE * NODES)
        nc.scalar.mul(out=bias_steep[:], in_=b2_turned[:, 0:C_TILES], mul=1.0 - SLOPE)
        nc.scalar.mul(out=bias_flat[:], in_=b2_turned[:, 0:C_TILES], mul=SLOPE)
        nc.scalar.copy(out=bias_whole[:], in_=b2_turned[:, 0:C_TILES])
        open_unit(units[1])
        add_pairs(units[1])
        quantise(units[0])
        leaky_and_round(units[1])
        for part in (1, 0):
            for half in range(HALVES):
                first_layer(part, 1, half, on_vector=False)
        for half in range(HALVES):
            turn_b(1, half)
            copy_b(1, half, nc.scalar.copy)
        open_unit(units[3], slots_of=0)
        add_pairs(units[3], 0, 1)
        quantise(units[1])
        leaky_and_round(units[2])
        add_pairs(units[3], 1, J_STEP)
        quantise(units[2])
        leaky_and_round(units[3])

        def spread(target, c_tile, start, stop):
            nc.tensor.matmul(
                out=target,
                lhsT=bias_sum[:, c_tile : c_tile + 1].to_broadcast([P, P]),
                rhs=identity[:],
                is_transpose=True,
                start=start,
                stop=stop,
            )

        out_rows = out.flatten_outer_dims()
        bank_pieces = {}
        leaky_pieces = {}

        last = STEPS - 1
        all_banks = list(range(PRODUCT_BANKS))
        early_banks = all_banks[: PRODUCT_BANKS // 2]
        late_banks = all_banks[PRODUCT_BANKS // 2 :]

        def output_tile(step, bank, k):
            return TILES_A_BANK * bank + k if step == last else bank + k * PRODUCT_BANKS

        def multiply(step, one_piece):
            codes, planes = h_words[step]
            bank_pieces[step] = []
            leaky_pieces[step] = []
            for bank in range(PRODUCT_BANKS):
                product = banks.tile([P, TILES_A_BANK, PAIRS], F32, tag="bank")
                steep = pieces.tile([P, TILES_A_BANK, PAIRS], F32, name="steep")
                flat = pieces.tile([P, TILES_A_BANK, PAIRS], F32, name="flat")
                for k in range(TILES_A_BANK):
                    c_tile = output_tile(step, bank, k)
                    m_cols = slice(c_tile * P, (c_tile + 1) * P)
                    for g in range(PASSES):
                        nc.tensor.matmul_mx(
                            out=product[:, k, :],
                            lhsT=w2_words[:, g, m_cols].bitcast(FP8X4),
                            lhsT_scale=w2_planes[4 * g : P, m_cols],
                            rhs=codes[:, g, :].bitcast(FP8X4),
                            rhs_scale=planes[:, g, :],
                            start=(g == 0),
                            stop=(g == PASSES - 1),
                        )
                if one_piece:
                    for k in range(TILES_A_BANK):
                        c_tile = output_tile(step, bank, k)
                        nc.scalar.activation(
                            out=flat[:, k, :],
                            in_=product[:, k, :],
                            func=ACT.Identity,
                            bias=bias_flat[:, c_tile : c_tile + 1],
                            scale=SLOPE,
                        )
                else:
                    nc.scalar.mul(out=flat[:], in_=product[:], mul=SLOPE)
                for k in range(TILES_A_BANK):
                    c_tile = output_tile(step, bank, k)
                    if one_piece:
                        nc.vector.scalar_tensor_tensor(
                            out=steep[:, k, :],
                            in0=product[:, k, :],
                            scalar=bias_whole[:, c_tile : c_tile + 1],
                            in1=flat[:, k, :],
                            op0=ALU.add,
                            op1=ALU.max,
                        )
                    else:
                        nc.scalar.activation(
                            out=steep[:, k, :],
                            in_=product[:, k, :],
                            func=ACT.Relu,
                            bias=bias_steep[:, c_tile : c_tile + 1],
                            scale=1.0 - SLOPE,
                        )
                bank_pieces[step].append((steep, flat))
                whole = (steep,) if one_piece else (steep, flat)
                leaky_pieces[step].append([[piece[:, half, :] for piece in whole] for half in range(HALVES)])

        def add_up(step, some_banks):
            r, of_tile = divmod(step, STEPS_A_TILE)
            for bank in some_banks:
                for half in range(HALVES):
                    pieces_here = leaky_pieces[step][bank][half]
                    for j in range(J_STEP):
                        for n, piece in enumerate(pieces_here):
                            nc.tensor.matmul(
                                out=sums[(r, half)][:, bank * P : (bank + 1) * P],
                                lhsT=piece[:, j * P : (j + 1) * P],
                                rhs=identity[:],
                                is_transpose=True,
                                start=(r == 1 and of_tile == 0 and bank == 0 and j == 0 and n == 0),
                                stop=(
                                    of_tile == STEPS_A_TILE - 1
                                    and bank == PRODUCT_BANKS - 1
                                    and j == J_STEP - 1
                                    and n == len(pieces_here) - 1
                                ),
                            )

        def store(r, half):
            result = results.tile([P, BANK], F32, name="result")
            if r == 0:
                nc.scalar.copy(out=result[:], in_=sums[(r, half)][:])
            else:
                nc.vector.scalar_tensor_tensor(
                    out=result[:],
                    in0=b2_everywhere[:, half * BANK : (half + 1) * BANK],
                    scalar=SLOPE * (NODES - J_STEP),
                    in1=sums[(r, half)][:],
                    op0=ALU.mult,
                    op1=ALU.add,
                )
            nc.sync.dma_start(out=out_rows[r * P : (r + 1) * P, half * BANK : (half + 1) * BANK], in_=result[:])

        tile_end = STEPS_A_TILE - 1

        def by_gpsimd(step):
            return 0 <= step < last - 3 and step != tile_end

        def join(step, bank, add):
            steep, flat = bank_pieces[step][bank]
            add(out=steep[:], in0=steep[:], in1=flat[:], op=ALU.add)
            leaky_pieces[step][bank] = [[steep[:, half, :]] for half in range(HALVES)]

        def sum_up(step):
            if by_gpsimd(step - 2):
                add_up(step - 2, all_banks[-1:])
            if step > 0:
                before = all_banks if step - 1 == tile_end + 1 else all_banks[1:] if step == last else late_banks
                add_up(step - 1, before[:-1] if by_gpsimd(step - 1) else before)
                if step - 1 == tile_end:
                    for half in range(HALVES):
                        store(0, half)
                        open_sum(1, half)
            if step < last and step != tile_end + 1:
                add_up(step, all_banks[:1] if step == last - 1 else early_banks)

        for half in range(HALVES):
            open_sum(0, half)
            for quarter in range(QUAD):
                spread(
                    sums[(0, half)][:, quarter * P : (quarter + 1) * P],
                    half * QUAD + quarter,
                    start=(quarter == 0),
                    stop=False,
                )
        multiply(0, one_piece=False)
        sum_up(0)
        for step in range(2, STEPS):
            first, second = (step, 0), (step, 1)
            open_unit(first)
            open_unit(second)
            add_pairs(first)
            together = 2 < step < last
            if together:
                add_pairs(second, 0, J_STEP - 1)
                add_pairs(second, J_STEP - 1, J_STEP, VECTOR_SETS)
                add_on_gpsimd(step)
                if by_gpsimd(step - 3):
                    join(step - 3, all_banks[-1], nc.gpsimd.tensor_tensor)
            if step == tile_end:
                for half in range(HALVES):
                    turn_a(1, half)
            quantise((step - 1, 1))
            multiply(step - 1, one_piece=False)
            sum_up(step - 1)
            leaky_and_round(first)
            if together:
                leaky_and_round(second)
                quantise(first)
            else:
                add_pairs(second)
                quantise(first)
                leaky_and_round(second)
        quantise((last, 1))
        for bank in all_banks[1:]:
            join(last - 1, bank, nc.vector.tensor_tensor)
        multiply(last, one_piece=True)
        sum_up(last)
        for bank in all_banks:
            for k in range(TILES_A_BANK):
                half, quarter = divmod(output_tile(last, bank, k), QUAD)
                (piece,) = leaky_pieces[last][bank][k]
                for j in range(J_STEP):
                    nc.tensor.matmul(
                        out=sums[(1, half)][:, quarter * P : (quarter + 1) * P],
                        lhsT=piece[:, j * P : (j + 1) * P],
                        rhs=identity[:],
                        is_transpose=True,
                        start=False,
                        stop=(quarter == QUAD - 1 and j == J_STEP - 1),
                    )
        for half in range(HALVES):
            store(1, half)
